import numpy as np
import ml_dtypes


def mxq(x, axis, fmt="e4m3"):
    dtype, down = {"e4m3": (ml_dtypes.float8_e4m3fn, 7), "e5m2": (ml_dtypes.float8_e5m2, 14)}[fmt]
    v = np.moveaxis(np.asarray(x, np.float32).astype(ml_dtypes.bfloat16).astype(np.float64), axis, -1)
    blocks = v.reshape(v.shape[:-1] + (-1, 32))
    amax = np.abs(blocks).max(-1, keepdims=True)
    byte = np.maximum(np.where(amax > 0, np.frexp(amax)[1] - 1 + 127, 0) - down, 1)
    scale = np.exp2(byte - 127.0)
    codes = (blocks / scale).astype(np.float32).astype(dtype).astype(np.float64)
    return np.moveaxis((codes * scale).reshape(v.shape), -1, axis)


WIDE = False


def mx_kscale(k):
    if not WIDE:
        return np.ones(k)
    levels = np.array([20, -20, 10, -10, 0])
    a = np.random.permutation(np.resize(levels, k // 512 * 4)).reshape(k // 512, 4)
    idx = np.arange(k)
    return np.exp2(a[idx // 512, idx % 128 // 32])


BF16 = ml_dtypes.bfloat16


def bf(x):
    return np.asarray(x, np.float32).astype(BF16)


def f64(x):
    return np.asarray(x).astype(np.float64)


B, DIN, H1, H2, N, I, K, O = 1024, 2048, 1024, 512, 32, 16, 256, 16
NI = N * I
KO = K * O
SQ_EPS = 1e-8
GSCALE = 64.0


def squash(t):
    sq = np.sum(t * t, axis=-1, keepdims=True)
    return (sq / (1.0 + sq)) * t / np.sqrt(sq + SQ_EPS)


def setup_inputs():
    u = mx_kscale(B)[:, None, None]
    p0 = bf(np.random.standard_normal((B, N, I)))
    Wr = bf(np.random.standard_normal((N, K, O, I)) * K / np.sqrt(NI * O))
    g = bf(np.random.standard_normal((B, K, O)) * np.exp2(np.random.randint(-12, 1, (B, 1, 1))) * GSCALE / u)
    wf = f64(Wr).transpose(0, 3, 1, 2).reshape(NI, KO)
    s = (f64(p0).reshape(B, NI) @ wf).reshape(B, K, O) * (1.0 / K)
    return {"p": bf(f64(p0) * u), "Wr": Wr, "s": np.asarray(s, np.float32), "grad_out": g}


def reference(p, Wr, s, grad_out):
    c = 1.0 / K
    sf = f64(s)
    gf = f64(grad_out)
    q = np.sum(sf * sf, axis=-1, keepdims=True)
    d = np.sum(gf * sf, axis=-1, keepdims=True)
    r = 1.0 / np.sqrt(q + SQ_EPS)
    a = q / (1.0 + q) * r
    e = r / ((1.0 + q) * (1.0 + q)) - 0.5 * q / (1.0 + q) * r * r * r
    ds = a * gf + 2.0 * e * d * sf
    pf = f64(p).reshape(B, NI)
    m = mxq(pf, 0, "e4m3").T @ mxq(ds.reshape(B, KO), 0, "e5m2")
    return m.reshape(N, I, K, O).transpose(0, 2, 3, 1) * c

@@ -1,0 +1,183 @@
+from contextlib import ExitStack
+
+import concourse.mybir as mybir
+from concourse.masks import make_identity
+
+F32 = mybir.dt.float32
+BF16 = mybir.dt.bfloat16
+U32 = mybir.dt.uint32
+U8 = mybir.dt.uint8
+E4M3X4 = mybir.dt.float8_e4m3fn_x4
+E5M2X4 = mybir.dt.float8_e5m2_x4
+ACT = mybir.ActivationFunctionType
+ALU = mybir.AluOpType
+AXIS_X = mybir.AxisListType.X
+
+P = 128
+PACK = 4
+BATCH = 1024
+PASSES = BATCH // (P * PACK)
+NI = 32 * 16
+CAP = 16
+COLS = 256 * CAP
+CHUNK = 512
+CHUNKS = COLS // CHUNK
+BLOCKS = CHUNK // P
+GROUPS = PACK * (CHUNK // CAP)
+SQ_EPS = 1e-8
+COUPLING = 1.0 / 256.0
+
+FLOPS = 2 * BATCH * NI * COLS
+BYTES = BATCH * NI * 2 + BATCH * COLS * (4 + 2) + NI * COLS * 4
+
+
+def by_capsule(tile):
+    return tile[:].rearrange("q t (j o) -> q (t j) o", o=CAP)
+
+
+def tile_capsulenetwork_pb_v_kernel(tc, p, Wr, s, grad_out, out):
+    nc = tc.nc
+    p_rows = p.rearrange("(h q t) n i -> h q t (n i)", h=PASSES, q=P, t=PACK)
+    s_rows = s.rearrange("(h q t) j o -> h q t (j o)", h=PASSES, q=P, t=PACK)
+    g_rows = grad_out.rearrange("(h q t) j o -> h q t (j o)", h=PASSES, q=P, t=PACK)
+    out_chunks = out.rearrange("n j o i -> n (j o i)").rearrange(
+        "n (c q x) -> c q n x", c=CHUNKS, q=P, x=BLOCKS * 16
+    )
+
+    with ExitStack() as stack:
+        const = stack.enter_context(tc.tile_pool(name="const", bufs=1))
+        stream = stack.enter_context(tc.tile_pool(name="stream", bufs=6))
+        work = stack.enter_context(tc.tile_pool(name="work", bufs=2))
+        small = stack.enter_context(tc.tile_pool(name="small", bufs=2))
+        factor_banks = stack.enter_context(tc.psum_pool(name="factor_banks", bufs=2))
+        product_banks = stack.enter_context(tc.psum_pool(name="product_banks", bufs=4))
+
+        identity = const.tile([P, P], F32)
+        make_identity(nc, identity[:])
+        eps = const.tile([P, 1], F32)
+        nc.vector.memset(eps[:], SQ_EPS)
+
+        p_raw = const.tile([P, PASSES, PACK, NI], BF16)
+        p_grouped = const.tile([P, PASSES, NI, PACK], BF16, align_bytes=64)
+        p_codes = const.tile([P, PASSES, NI], U32, align_bytes=64)
+        p_scales = const.tile([P, PASSES, NI], U8, align_bytes=64)
+        for h in range(PASSES):
+            nc.scalar.dma_start(out=p_raw[:, h], in_=p_rows[h])
+            nc.vector.tensor_copy(out=p_grouped[:, h], in_=p_raw[:, h].rearrange("q t w -> q w t"))
+        nc.vector.quantize_mx(
+            out=p_codes[:].rearrange("q h w -> q (h w)").bitcast(E4M3X4),
+            scales=p_scales[:].rearrange("q h w -> q (h w)"),
+            in_=p_grouped[:].rearrange("q h w t -> q (h w t)"),
+        )
+
+        for c in range(CHUNKS):
+            cols = slice(c * CHUNK, (c + 1) * CHUNK)
+
+            q = small.tile([P, PASSES * GROUPS], F32)
+            d = small.tile([P, PASSES * GROUPS], F32)
+            s_tiles = []
+            g_tiles = []
+            for h in range(PASSES):
+                groups = slice(h * GROUPS, (h + 1) * GROUPS)
+                s_t = stream.tile([P, PACK, CHUNK], F32)
+                nc.sync.dma_start(out=s_t[:], in_=s_rows[h, :, :, cols])
+                g_t = stream.tile([P, PACK, CHUNK], BF16)
+                nc.sync.dma_start(out=g_t[:], in_=g_rows[h, :, :, cols])
+                s_tiles.append(s_t)
+                g_tiles.append(g_t)
+                squares = work.tile([P, PACK, CHUNK], F32)
+                nc.scalar.activation(out=squares[:], in_=s_t[:], func=ACT.Square)
+                g_times_s = work.tile([P, PACK, CHUNK], F32)
+                nc.gpsimd.tensor_tensor(out=g_times_s[:], in0=g_t[:], in1=s_t[:], op=ALU.mult)
+                nc.vector.tensor_reduce(out=q[:, groups], in_=by_capsule(squares), axis=AXIS_X, op=ALU.add)
+                nc.vector.tensor_reduce(out=d[:, groups], in_=by_capsule(g_times_s), axis=AXIS_X, op=ALU.add)
+
+            factors = small.tile([P, 2, PASSES * GROUPS], F32)
+            root = small.tile([P, PASSES * GROUPS], F32)
+            nc.scalar.activation(out=root[:], in_=q[:], func=ACT.Sqrt, bias=eps[:, 0:1])
+            q_squared = small.tile([P, PASSES * GROUPS], F32)
+            nc.scalar.activation(out=q_squared[:], in_=q[:], func=ACT.Square)
+            denominator = small.tile([P, PASSES * GROUPS], F32)
+            nc.vector.scalar_tensor_tensor(
+                out=denominator[:], in0=q[:], scalar=1.0, in1=root[:], op0=ALU.add, op1=ALU.mult
+            )
+            z = small.tile([P, PASSES * GROUPS], F32)
+            nc.vector.reciprocal(out=z[:], in_=denominator[:])
+            z_squared = small.tile([P, PASSES * GROUPS], F32)
+            nc.scalar.activation(out=z_squared[:], in_=z[:], func=ACT.Square)
+            nc.vector.tensor_tensor(out=factors[:, 0, :], in0=q[:], in1=z[:], op=ALU.mult)
+            numerator = small.tile([P, PASSES * GROUPS], F32)
+            nc.vector.scalar_tensor_tensor(
+                out=numerator[:], in0=q[:], scalar=2.0 * SQ_EPS, in1=q_squared[:], op0=ALU.add, op1=ALU.subtract
+            )
+            polynomial = small.tile([P, PASSES * GROUPS], F32)
+            nc.vector.scalar_tensor_tensor(
+                out=polynomial[:], in0=q[:], scalar=1.0, in1=numerator[:], op0=ALU.add, op1=ALU.mult
+            )
+            z2_poly = small.tile([P, PASSES * GROUPS], F32)
+            nc.vector.tensor_tensor(out=z2_poly[:], in0=z_squared[:], in1=polynomial[:], op=ALU.mult)
+            z_d = small.tile([P, PASSES * GROUPS], F32)
+            nc.vector.tensor_tensor(out=z_d[:], in0=z[:], in1=d[:], op=ALU.mult)
+            nc.vector.tensor_tensor(out=factors[:, 1, :], in0=z2_poly[:], in1=z_d[:], op=ALU.mult)
+
+            factors_psum = factor_banks.tile([P, 2, PASSES * GROUPS], F32)
+            nc.tensor.matmul(
+                out=factors_psum[:].rearrange("q k x -> q (k x)"),
+                lhsT=identity[:],
+                rhs=factors[:].rearrange("q k x -> q (k x)"),
+                start=True,
+                stop=True,
+            )
+
+            ds_codes = work.tile([P, PASSES, CHUNK], U32, align_bytes=64)
+            ds_scales = work.tile([P, PASSES, CHUNK], U8, align_bytes=64)
+            for h in range(PASSES):
+                groups = slice(h * GROUPS, (h + 1) * GROUPS)
+                s_t = s_tiles[h]
+                g_t = g_tiles[h]
+                a_g = work.tile([P, PACK, CHUNK], F32)
+                nc.vector.tensor_tensor(
+                    out=by_capsule(a_g),
+                    in0=by_capsule(g_t),
+                    in1=factors_psum[:, 0, groups].unsqueeze(2).to_broadcast([P, GROUPS, CAP]),
+                    op=ALU.mult,
+                )
+                nc.vector.tensor_tensor(
+                    out=by_capsule(s_t),
+                    in0=by_capsule(s_t),
+                    in1=factors_psum[:, 1, groups].unsqueeze(2).to_broadcast([P, GROUPS, CAP]),
+                    op=ALU.mult,
+                )
+                ds = work.tile([P, PACK, CHUNK], BF16)
+                nc.gpsimd.tensor_tensor(out=ds[:], in0=a_g[:], in1=s_t[:], op=ALU.add)
+                ds_grouped = work.tile([P, CHUNK, PACK], BF16, align_bytes=64)
+                nc.scalar.copy(
+                    out=ds_grouped[:].rearrange("q (m w) t -> q m w t", m=BLOCKS),
+                    in_=ds[:].rearrange("q t (w m) -> q m w t", m=BLOCKS),
+                )
+                nc.vector.quantize_mx(
+                    out=ds_codes[:, h, :].bitcast(E5M2X4),
+                    scales=ds_scales[:, h, :],
+                    in_=ds_grouped[:].rearrange("q w t -> q (w t)"),
+                )
+
+            result = work.tile([P, 32, BLOCKS, 16], F32)
+            for m in range(BLOCKS):
+                block = slice(m * P, (m + 1) * P)
+                product = product_banks.tile([P, NI], F32)
+                for h in range(PASSES):
+                    nc.tensor.matmul_mx(
+                        out=product[:],
+                        lhsT=ds_codes[:, h, block].bitcast(E5M2X4),
+                        lhsT_scale=ds_scales[:, h, block],
+                        rhs=p_codes[:, h, :].bitcast(E4M3X4),
+                        rhs_scale=p_scales[:, h, :],
+                        start=(h == 0),
+                        stop=(h == PASSES - 1),
+                    )
+                nc.scalar.mul(
+                    out=result[:, :, m, :],
+                    in_=product[:].rearrange("q (n i) -> q n i", i=16),
+                    mul=COUPLING,
+                )
+            nc.scalar.dma_start(out=out_chunks[c], in_=result[:].rearrange("q n m i -> q n (m i)"))

@@ -43,6 +43,7 @@ def tile_capsulenetwork_pb_v_kernel(tc, p, Wr, s, grad_out, out):
     out_chunks = out.rearrange("n j o i -> n (j o i)").rearrange(
         "n (c q x) -> c q n x", c=CHUNKS, q=P, x=BLOCKS * 16
     )
+    halves = range(PASSES)
 
     with ExitStack() as stack:
         const = stack.enter_context(tc.tile_pool(name="const", bufs=1))
@@ -51,101 +52,144 @@ def tile_capsulenetwork_pb_v_kernel(tc, p, Wr, s, grad_out, out):
         small = stack.enter_context(tc.tile_pool(name="small", bufs=2))
         factor_banks = stack.enter_context(tc.psum_pool(name="factor_banks", bufs=2))
         product_banks = stack.enter_context(tc.psum_pool(name="product_banks", bufs=4))
+        stack.enter_context(tc.manual_schedule())
+
+        s_of = {}
+        g_of = {}
+        squares_of = {}
+        g_times_s_of = {}
+        q_of = {}
+        root_of = {}
+        q_squared_of = {}
+        d_of = {}
+        factors_of = {}
+        grouped_of = {}
+        codes_of = {}
+        scales_of = {}
 
         identity = const.tile([P, P], F32)
         make_identity(nc, identity[:])
         eps = const.tile([P, 1], F32)
         nc.vector.memset(eps[:], SQ_EPS)
-
         p_raw = const.tile([P, PASSES, PACK, NI], BF16)
         p_grouped = const.tile([P, PASSES, NI, PACK], BF16, align_bytes=64)
         p_codes = const.tile([P, PASSES, NI], U32, align_bytes=64)
         p_scales = const.tile([P, PASSES, NI], U8, align_bytes=64)
-        for h in range(PASSES):
-            nc.scalar.dma_start(out=p_raw[:, h], in_=p_rows[h])
-            nc.vector.tensor_copy(out=p_grouped[:, h], in_=p_raw[:, h].rearrange("q t w -> q w t"))
-        nc.vector.quantize_mx(
-            out=p_codes[:].rearrange("q h w -> q (h w)").bitcast(E4M3X4),
-            scales=p_scales[:].rearrange("q h w -> q (h w)"),
-            in_=p_grouped[:].rearrange("q h w t -> q (h w t)"),
-        )
 
-        for c in range(CHUNKS):
+        def load(c):
             cols = slice(c * CHUNK, (c + 1) * CHUNK)
-
-            q = small.tile([P, PASSES * GROUPS], F32)
-            d = small.tile([P, PASSES * GROUPS], F32)
-            s_tiles = []
-            g_tiles = []
-            for h in range(PASSES):
-                groups = slice(h * GROUPS, (h + 1) * GROUPS)
+            for h in halves:
                 s_t = stream.tile([P, PACK, CHUNK], F32)
                 nc.sync.dma_start(out=s_t[:], in_=s_rows[h, :, :, cols])
                 g_t = stream.tile([P, PACK, CHUNK], BF16)
                 nc.sync.dma_start(out=g_t[:], in_=g_rows[h, :, :, cols])
-                s_tiles.append(s_t)
-                g_tiles.append(g_t)
-                squares = work.tile([P, PACK, CHUNK], F32)
-                nc.scalar.activation(out=squares[:], in_=s_t[:], func=ACT.Square)
-                g_times_s = work.tile([P, PACK, CHUNK], F32)
-                nc.gpsimd.tensor_tensor(out=g_times_s[:], in0=g_t[:], in1=s_t[:], op=ALU.mult)
-                nc.vector.tensor_reduce(out=q[:, groups], in_=by_capsule(squares), axis=AXIS_X, op=ALU.add)
-                nc.vector.tensor_reduce(out=d[:, groups], in_=by_capsule(g_times_s), axis=AXIS_X, op=ALU.add)
+                s_of[(c, h)] = s_t
+                g_of[(c, h)] = g_t
 
-            factors = small.tile([P, 2, PASSES * GROUPS], F32)
+        def quantise_p():
+            for h in halves:
+                nc.vector.tensor_copy(out=p_grouped[:, h], in_=p_raw[:, h].rearrange("q t w -> q w t"))
+            nc.vector.quantize_mx(
+                out=p_codes[:].rearrange("q h w -> q (h w)").bitcast(E4M3X4),
+                scales=p_scales[:].rearrange("q h w -> q (h w)"),
+                in_=p_grouped[:].rearrange("q h w t -> q (h w t)"),
+            )
+
+        def square(c):
+            for h in halves:
+                squares = work.tile([P, PACK, CHUNK], F32)
+                nc.scalar.activation(out=squares[:], in_=s_of[(c, h)][:], func=ACT.Square)
+                squares_of[(c, h)] = squares
+
+        def multiply_g_s(c):
+            for h in halves:
+                g_times_s = work.tile([P, PACK, CHUNK], F32)
+                nc.gpsimd.tensor_tensor(
+                    out=g_times_s[:], in0=g_of[(c, h)][:], in1=s_of[(c, h)][:], op=ALU.mult
+                )
+                g_times_s_of[(c, h)] = g_times_s
+
+        def sum_squares(c):
+            q = small.tile([P, PASSES * GROUPS], F32)
+            for h in halves:
+                nc.vector.tensor_reduce(
+                    out=q[:, h * GROUPS : (h + 1) * GROUPS],
+                    in_=by_capsule(squares_of[(c, h)]),
+                    axis=AXIS_X,
+                    op=ALU.add,
+                )
             root = small.tile([P, PASSES * GROUPS], F32)
             nc.scalar.activation(out=root[:], in_=q[:], func=ACT.Sqrt, bias=eps[:, 0:1])
             q_squared = small.tile([P, PASSES * GROUPS], F32)
             nc.scalar.activation(out=q_squared[:], in_=q[:], func=ACT.Square)
-            denominator = small.tile([P, PASSES * GROUPS], F32)
+            q_of[c] = q
+            root_of[c] = root
+            q_squared_of[c] = q_squared
+
+        def sum_products(c):
+            d = small.tile([P, PASSES * GROUPS], F32)
+            for h in halves:
+                nc.vector.tensor_reduce(
+                    out=d[:, h * GROUPS : (h + 1) * GROUPS],
+                    in_=by_capsule(g_times_s_of[(c, h)]),
+                    axis=AXIS_X,
+                    op=ALU.add,
+                )
+            d_of[c] = d
+
+        def factors(c):
+            q = q_of[c]
+            d = d_of[c]
+            width = [P, PASSES * GROUPS]
+            denominator = small.tile(width, F32)
             nc.vector.scalar_tensor_tensor(
-                out=denominator[:], in0=q[:], scalar=1.0, in1=root[:], op0=ALU.add, op1=ALU.mult
+                out=denominator[:], in0=q[:], scalar=1.0, in1=root_of[c][:], op0=ALU.add, op1=ALU.mult
             )
-            z = small.tile([P, PASSES * GROUPS], F32)
+            numerator = small.tile(width, F32)
+            nc.vector.scalar_tensor_tensor(
+                out=numerator[:], in0=q[:], scalar=2.0 * SQ_EPS, in1=q_squared_of[c][:],
+                op0=ALU.add, op1=ALU.subtract,
+            )
+            z = small.tile(width, F32)
             nc.vector.reciprocal(out=z[:], in_=denominator[:])
-            z_squared = small.tile([P, PASSES * GROUPS], F32)
-            nc.scalar.activation(out=z_squared[:], in_=z[:], func=ACT.Square)
-            nc.vector.tensor_tensor(out=factors[:, 0, :], in0=q[:], in1=z[:], op=ALU.mult)
-            numerator = small.tile([P, PASSES * GROUPS], F32)
-            nc.vector.scalar_tensor_tensor(
-                out=numerator[:], in0=q[:], scalar=2.0 * SQ_EPS, in1=q_squared[:], op0=ALU.add, op1=ALU.subtract
-            )
-            polynomial = small.tile([P, PASSES * GROUPS], F32)
+            polynomial = small.tile(width, F32)
             nc.vector.scalar_tensor_tensor(
                 out=polynomial[:], in0=q[:], scalar=1.0, in1=numerator[:], op0=ALU.add, op1=ALU.mult
             )
-            z2_poly = small.tile([P, PASSES * GROUPS], F32)
-            nc.vector.tensor_tensor(out=z2_poly[:], in0=z_squared[:], in1=polynomial[:], op=ALU.mult)
-            z_d = small.tile([P, PASSES * GROUPS], F32)
+            z_d = small.tile(width, F32)
             nc.vector.tensor_tensor(out=z_d[:], in0=z[:], in1=d[:], op=ALU.mult)
-            nc.vector.tensor_tensor(out=factors[:, 1, :], in0=z2_poly[:], in1=z_d[:], op=ALU.mult)
-
-            factors_psum = factor_banks.tile([P, 2, PASSES * GROUPS], F32)
+            z_poly = small.tile(width, F32)
+            nc.vector.tensor_tensor(out=z_poly[:], in0=z[:], in1=polynomial[:], op=ALU.mult)
+            zz_d = small.tile(width, F32)
+            nc.vector.tensor_tensor(out=zz_d[:], in0=z[:], in1=z_d[:], op=ALU.mult)
+            a_beta = small.tile([P, 2, PASSES * GROUPS], F32)
+            nc.vector.tensor_tensor(out=a_beta[:, 0, :], in0=q[:], in1=z[:], op=ALU.mult)
+            nc.vector.tensor_tensor(out=a_beta[:, 1, :], in0=z_poly[:], in1=zz_d[:], op=ALU.mult)
+            a_beta_psum = factor_banks.tile([P, 2, PASSES * GROUPS], F32)
             nc.tensor.matmul(
-                out=factors_psum[:].rearrange("q k x -> q (k x)"),
+                out=a_beta_psum[:].rearrange("q k x -> q (k x)"),
                 lhsT=identity[:],
-                rhs=factors[:].rearrange("q k x -> q (k x)"),
+                rhs=a_beta[:].rearrange("q k x -> q (k x)"),
                 start=True,
                 stop=True,
             )
+            factors_of[c] = a_beta_psum
 
-            ds_codes = work.tile([P, PASSES, CHUNK], U32, align_bytes=64)
-            ds_scales = work.tile([P, PASSES, CHUNK], U8, align_bytes=64)
-            for h in range(PASSES):
+        def scale_and_add(c):
+            for h in halves:
                 groups = slice(h * GROUPS, (h + 1) * GROUPS)
-                s_t = s_tiles[h]
-                g_t = g_tiles[h]
+                s_t = s_of[(c, h)]
                 a_g = work.tile([P, PACK, CHUNK], F32)
                 nc.vector.tensor_tensor(
                     out=by_capsule(a_g),
-                    in0=by_capsule(g_t),
-                    in1=factors_psum[:, 0, groups].unsqueeze(2).to_broadcast([P, GROUPS, CAP]),
+                    in0=by_capsule(g_of[(c, h)]),
+                    in1=factors_of[c][:, 0, groups].unsqueeze(2).to_broadcast([P, GROUPS, CAP]),
                     op=ALU.mult,
                 )
                 nc.vector.tensor_tensor(
                     out=by_capsule(s_t),
                     in0=by_capsule(s_t),
-                    in1=factors_psum[:, 1, groups].unsqueeze(2).to_broadcast([P, GROUPS, CAP]),
+                    in1=factors_of[c][:, 1, groups].unsqueeze(2).to_broadcast([P, GROUPS, CAP]),
                     op=ALU.mult,
                 )
                 ds = work.tile([P, PACK, CHUNK], BF16)
@@ -155,21 +199,30 @@ def tile_capsulenetwork_pb_v_kernel(tc, p, Wr, s, grad_out, out):
                     out=ds_grouped[:].rearrange("q (m w) t -> q m w t", m=BLOCKS),
                     in_=ds[:].rearrange("q t (w m) -> q m w t", m=BLOCKS),
                 )
-                nc.vector.quantize_mx(
-                    out=ds_codes[:, h, :].bitcast(E5M2X4),
-                    scales=ds_scales[:, h, :],
-                    in_=ds_grouped[:].rearrange("q w t -> q (w t)"),
-                )
+                grouped_of[(c, h)] = ds_grouped
 
+        def quantise(c, h):
+            if h == 0:
+                ds_codes = work.tile([P, PASSES, CHUNK], U32, align_bytes=64)
+                ds_scales = work.tile([P, PASSES, CHUNK], U8, align_bytes=64)
+                codes_of[c] = ds_codes
+                scales_of[c] = ds_scales
+            nc.vector.quantize_mx(
+                out=codes_of[c][:, h, :].bitcast(E5M2X4),
+                scales=scales_of[c][:, h, :],
+                in_=grouped_of[(c, h)][:].rearrange("q w t -> q (w t)"),
+            )
+
+        def multiply(c):
             result = work.tile([P, 32, BLOCKS, 16], F32)
             for m in range(BLOCKS):
                 block = slice(m * P, (m + 1) * P)
                 product = product_banks.tile([P, NI], F32)
-                for h in range(PASSES):
+                for h in halves:
                     nc.tensor.matmul_mx(
                         out=product[:],
-                        lhsT=ds_codes[:, h, block].bitcast(E5M2X4),
-                        lhsT_scale=ds_scales[:, h, block],
+                        lhsT=codes_of[c][:, h, block].bitcast(E5M2X4),
+                        lhsT_scale=scales_of[c][:, h, block],
                         rhs=p_codes[:, h, :].bitcast(E4M3X4),
                         rhs_scale=p_scales[:, h, :],
                         start=(h == 0),
@@ -180,4 +233,35 @@ def tile_capsulenetwork_pb_v_kernel(tc, p, Wr, s, grad_out, out):
                     in_=product[:].rearrange("q (n i) -> q n i", i=16),
                     mul=COUPLING,
                 )
-            nc.scalar.dma_start(out=out_chunks[c], in_=result[:].rearrange("q n m i -> q n (m i)"))
+            nc.sync.dma_start(out=out_chunks[c], in_=result[:].rearrange("q n m i -> q n (m i)"))
+
+        load(0)
+        for h in halves:
+            nc.sync.dma_start(out=p_raw[:, h], in_=p_rows[h])
+        load(1)
+        load(2)
+        square(0)
+        multiply_g_s(0)
+        sum_squares(0)
+        quantise_p()
+        square(1)
+        for c in range(CHUNKS):
+            sum_products(c)
+            if c + 1 < CHUNKS:
+                multiply_g_s(c + 1)
+            if c >= 1:
+                quantise(c - 1, 0)
+            factors(c)
+            if c >= 1:
+                quantise(c - 1, 1)
+                multiply(c - 1)
+            if c + 1 < CHUNKS:
+                sum_squares(c + 1)
+            if c + 2 < CHUNKS:
+                square(c + 2)
+            scale_and_add(c)
+            if c + 3 < CHUNKS:
+                load(c + 3)
+        quantise(CHUNKS - 1, 0)
+        quantise(CHUNKS - 1, 1)
+        multiply(CHUNKS - 1)

@@ -44,10 +44,11 @@ def tile_capsulenetwork_pb_v_kernel(tc, p, Wr, s, grad_out, out):
         "n (c q x) -> c q n x", c=CHUNKS, q=P, x=BLOCKS * 16
     )
     halves = range(PASSES)
+    per_capsule = [P, PASSES * GROUPS]
 
     with ExitStack() as stack:
         const = stack.enter_context(tc.tile_pool(name="const", bufs=1))
-        stream = stack.enter_context(tc.tile_pool(name="stream", bufs=6))
+        stream = stack.enter_context(tc.tile_pool(name="stream", bufs=8))
         work = stack.enter_context(tc.tile_pool(name="work", bufs=2))
         small = stack.enter_context(tc.tile_pool(name="small", bufs=2))
         factor_banks = stack.enter_context(tc.psum_pool(name="factor_banks", bufs=2))
@@ -62,7 +63,11 @@ def tile_capsulenetwork_pb_v_kernel(tc, p, Wr, s, grad_out, out):
         root_of = {}
         q_squared_of = {}
         d_of = {}
+        numerator_of = {}
+        z_of = {}
         factors_of = {}
+        a_g_of = {}
+        ds_of = {}
         grouped_of = {}
         codes_of = {}
         scales_of = {}
@@ -71,8 +76,6 @@ def tile_capsulenetwork_pb_v_kernel(tc, p, Wr, s, grad_out, out):
         make_identity(nc, identity[:])
         eps = const.tile([P, 1], F32)
         nc.vector.memset(eps[:], SQ_EPS)
-        p_raw = const.tile([P, PASSES, PACK, NI], BF16)
-        p_grouped = const.tile([P, PASSES, NI, PACK], BF16, align_bytes=64)
         p_codes = const.tile([P, PASSES, NI], U32, align_bytes=64)
         p_scales = const.tile([P, PASSES, NI], U8, align_bytes=64)
 
@@ -85,15 +88,6 @@ def tile_capsulenetwork_pb_v_kernel(tc, p, Wr, s, grad_out, out):
                 nc.sync.dma_start(out=g_t[:], in_=g_rows[h, :, :, cols])
                 s_of[(c, h)] = s_t
                 g_of[(c, h)] = g_t
-
-        def quantise_p():
-            for h in halves:
-                nc.vector.tensor_copy(out=p_grouped[:, h], in_=p_raw[:, h].rearrange("q t w -> q w t"))
-            nc.vector.quantize_mx(
-                out=p_codes[:].rearrange("q h w -> q (h w)").bitcast(E4M3X4),
-                scales=p_scales[:].rearrange("q h w -> q (h w)"),
-                in_=p_grouped[:].rearrange("q h w t -> q (h w t)"),
-            )
 
         def square(c):
             for h in halves:
@@ -110,7 +104,7 @@ def tile_capsulenetwork_pb_v_kernel(tc, p, Wr, s, grad_out, out):
                 g_times_s_of[(c, h)] = g_times_s
 
         def sum_squares(c):
-            q = small.tile([P, PASSES * GROUPS], F32)
+            q = small.tile(per_capsule, F32)
             for h in halves:
                 nc.vector.tensor_reduce(
                     out=q[:, h * GROUPS : (h + 1) * GROUPS],
@@ -118,16 +112,16 @@ def tile_capsulenetwork_pb_v_kernel(tc, p, Wr, s, grad_out, out):
                     axis=AXIS_X,
                     op=ALU.add,
                 )
-            root = small.tile([P, PASSES * GROUPS], F32)
+            root = small.tile(per_capsule, F32)
             nc.scalar.activation(out=root[:], in_=q[:], func=ACT.Sqrt, bias=eps[:, 0:1])
-            q_squared = small.tile([P, PASSES * GROUPS], F32)
+            q_squared = small.tile(per_capsule, F32)
             nc.scalar.activation(out=q_squared[:], in_=q[:], func=ACT.Square)
             q_of[c] = q
             root_of[c] = root
             q_squared_of[c] = q_squared
 
         def sum_products(c):
-            d = small.tile([P, PASSES * GROUPS], F32)
+            d = small.tile(per_capsule, F32)
             for h in halves:
                 nc.vector.tensor_reduce(
                     out=d[:, h * GROUPS : (h + 1) * GROUPS],
@@ -137,30 +131,35 @@ def tile_capsulenetwork_pb_v_kernel(tc, p, Wr, s, grad_out, out):
                 )
             d_of[c] = d
 
-        def factors(c):
+
+        def start_factors(c):
             q = q_of[c]
-            d = d_of[c]
-            width = [P, PASSES * GROUPS]
-            denominator = small.tile(width, F32)
+            denominator = small.tile(per_capsule, F32)
             nc.vector.scalar_tensor_tensor(
                 out=denominator[:], in0=q[:], scalar=1.0, in1=root_of[c][:], op0=ALU.add, op1=ALU.mult
             )
-            numerator = small.tile(width, F32)
+            numerator = small.tile(per_capsule, F32)
             nc.vector.scalar_tensor_tensor(
                 out=numerator[:], in0=q[:], scalar=2.0 * SQ_EPS, in1=q_squared_of[c][:],
                 op0=ALU.add, op1=ALU.subtract,
             )
-            z = small.tile(width, F32)
+            z = small.tile(per_capsule, F32)
             nc.vector.reciprocal(out=z[:], in_=denominator[:])
-            polynomial = small.tile(width, F32)
+            numerator_of[c] = numerator
+            z_of[c] = z
+
+        def finish_factors(c):
+            q = q_of[c]
+            z = z_of[c]
+            polynomial = small.tile(per_capsule, F32)
             nc.vector.scalar_tensor_tensor(
-                out=polynomial[:], in0=q[:], scalar=1.0, in1=numerator[:], op0=ALU.add, op1=ALU.mult
+                out=polynomial[:], in0=q[:], scalar=1.0, in1=numerator_of[c][:], op0=ALU.add, op1=ALU.mult
             )
-            z_d = small.tile(width, F32)
-            nc.vector.tensor_tensor(out=z_d[:], in0=z[:], in1=d[:], op=ALU.mult)
-            z_poly = small.tile(width, F32)
+            z_d = small.tile(per_capsule, F32)
+            nc.vector.tensor_tensor(out=z_d[:], in0=z[:], in1=d_of[c][:], op=ALU.mult)
+            z_poly = small.tile(per_capsule, F32)
             nc.vector.tensor_tensor(out=z_poly[:], in0=z[:], in1=polynomial[:], op=ALU.mult)
-            zz_d = small.tile(width, F32)
+            zz_d = small.tile(per_capsule, F32)
             nc.vector.tensor_tensor(out=zz_d[:], in0=z[:], in1=z_d[:], op=ALU.mult)
             a_beta = small.tile([P, 2, PASSES * GROUPS], F32)
             nc.vector.tensor_tensor(out=a_beta[:, 0, :], in0=q[:], in1=z[:], op=ALU.mult)
@@ -175,46 +174,50 @@ def tile_capsulenetwork_pb_v_kernel(tc, p, Wr, s, grad_out, out):
             )
             factors_of[c] = a_beta_psum
 
-        def scale_and_add(c):
-            for h in halves:
-                groups = slice(h * GROUPS, (h + 1) * GROUPS)
-                s_t = s_of[(c, h)]
-                a_g = work.tile([P, PACK, CHUNK], F32)
-                nc.vector.tensor_tensor(
-                    out=by_capsule(a_g),
-                    in0=by_capsule(g_of[(c, h)]),
-                    in1=factors_of[c][:, 0, groups].unsqueeze(2).to_broadcast([P, GROUPS, CAP]),
-                    op=ALU.mult,
-                )
-                nc.vector.tensor_tensor(
-                    out=by_capsule(s_t),
-                    in0=by_capsule(s_t),
-                    in1=factors_of[c][:, 1, groups].unsqueeze(2).to_broadcast([P, GROUPS, CAP]),
-                    op=ALU.mult,
-                )
-                ds = work.tile([P, PACK, CHUNK], BF16)
-                nc.gpsimd.tensor_tensor(out=ds[:], in0=a_g[:], in1=s_t[:], op=ALU.add)
-                ds_grouped = work.tile([P, CHUNK, PACK], BF16, align_bytes=64)
-                nc.scalar.copy(
-                    out=ds_grouped[:].rearrange("q (m w) t -> q m w t", m=BLOCKS),
-                    in_=ds[:].rearrange("q t (w m) -> q m w t", m=BLOCKS),
-                )
-                grouped_of[(c, h)] = ds_grouped
-
-        def quantise(c, h):
-            if h == 0:
-                ds_codes = work.tile([P, PASSES, CHUNK], U32, align_bytes=64)
-                ds_scales = work.tile([P, PASSES, CHUNK], U8, align_bytes=64)
-                codes_of[c] = ds_codes
-                scales_of[c] = ds_scales
-            nc.vector.quantize_mx(
-                out=codes_of[c][:, h, :].bitcast(E5M2X4),
-                scales=scales_of[c][:, h, :],
-                in_=grouped_of[(c, h)][:].rearrange("q w t -> q (w t)"),
+        def scale(c, h):
+            groups = slice(h * GROUPS, (h + 1) * GROUPS)
+            a_g = work.tile([P, PACK, CHUNK], F32)
+            nc.vector.tensor_tensor(
+                out=by_capsule(a_g),
+                in0=by_capsule(g_of[(c, h)]),
+                in1=factors_of[c][:, 0, groups].unsqueeze(2).to_broadcast([P, GROUPS, CAP]),
+                op=ALU.mult,
             )
+            nc.vector.tensor_tensor(
+                out=by_capsule(s_of[(c, h)]),
+                in0=by_capsule(s_of[(c, h)]),
+                in1=factors_of[c][:, 1, groups].unsqueeze(2).to_broadcast([P, GROUPS, CAP]),
+                op=ALU.mult,
+            )
+            a_g_of[(c, h)] = a_g
 
-        def multiply(c):
-            result = work.tile([P, 32, BLOCKS, 16], F32)
+        def add(c, h):
+            ds = work.tile([P, PACK, CHUNK], BF16)
+            nc.gpsimd.tensor_tensor(out=ds[:], in0=a_g_of[(c, h)][:], in1=s_of[(c, h)][:], op=ALU.add)
+            ds_of[(c, h)] = ds
+
+        def regroup(c, h):
+            ds_grouped = work.tile([P, CHUNK, PACK], BF16, align_bytes=64)
+            nc.scalar.copy(
+                out=ds_grouped[:].rearrange("q (m w) t -> q m w t", m=BLOCKS),
+                in_=ds_of[(c, h)][:].rearrange("q t (w m) -> q m w t", m=BLOCKS),
+            )
+            grouped_of[(c, h)] = ds_grouped
+
+        def quantise(c):
+            ds_codes = work.tile([P, PASSES, CHUNK], U32, align_bytes=64)
+            ds_scales = work.tile([P, PASSES, CHUNK], U8, align_bytes=64)
+            for h in halves:
+                nc.vector.quantize_mx(
+                    out=ds_codes[:, h, :].bitcast(E5M2X4),
+                    scales=ds_scales[:, h, :],
+                    in_=grouped_of[(c, h)][:].rearrange("q w t -> q (w t)"),
+                )
+            codes_of[c] = ds_codes
+            scales_of[c] = ds_scales
+
+        def multiply(c, results):
+            result = results.tile([P, 32, BLOCKS, 16], F32)
             for m in range(BLOCKS):
                 block = slice(m * P, (m + 1) * P)
                 product = product_banks.tile([P, NI], F32)
@@ -236,32 +239,49 @@ def tile_capsulenetwork_pb_v_kernel(tc, p, Wr, s, grad_out, out):
             nc.sync.dma_start(out=out_chunks[c], in_=result[:].rearrange("q n m i -> q n (m i)"))
 
         load(0)
-        for h in halves:
-            nc.sync.dma_start(out=p_raw[:, h], in_=p_rows[h])
-        load(1)
-        load(2)
-        square(0)
-        multiply_g_s(0)
-        sum_squares(0)
-        quantise_p()
+        with tc.tile_pool(name="p_stage", bufs=1) as p_stage:
+            p_raw = p_stage.tile([P, PASSES, PACK, NI], BF16)
+            p_grouped = p_stage.tile([P, PASSES, NI, PACK], BF16, align_bytes=64)
+            for h in halves:
+                nc.sync.dma_start(out=p_raw[:, h], in_=p_rows[h])
+            load(1)
+            square(0)
+            sum_squares(0)
+            multiply_g_s(0)
+            for h in halves:
+                nc.vector.tensor_copy(out=p_grouped[:, h], in_=p_raw[:, h].rearrange("q t w -> q w t"))
+            nc.vector.quantize_mx(
+                out=p_codes[:].rearrange("q h w -> q (h w)").bitcast(E4M3X4),
+                scales=p_scales[:].rearrange("q h w -> q (h w)"),
+                in_=p_grouped[:].rearrange("q h w t -> q (h w t)"),
+            )
+        results = stack.enter_context(tc.tile_pool(name="results", bufs=2))
+        start_factors(0)
         square(1)
-        for c in range(CHUNKS):
-            sum_products(c)
+        load(2)
+
+        for c in range(-1, CHUNKS):
+            if c >= 0:
+                for h in halves:
+                    scale(c, h)
+                    add(c, h)
             if c + 1 < CHUNKS:
-                multiply_g_s(c + 1)
-            if c >= 1:
-                quantise(c - 1, 0)
-            factors(c)
-            if c >= 1:
-                quantise(c - 1, 1)
-                multiply(c - 1)
-            if c + 1 < CHUNKS:
-                sum_squares(c + 1)
+                sum_products(c + 1)
+            if c + 4 < CHUNKS:
+                load(c + 4)
+            if c >= 0:
+                for h in halves:
+                    regroup(c, h)
             if c + 2 < CHUNKS:
-                square(c + 2)
-            scale_and_add(c)
+                sum_squares(c + 2)
+                multiply_g_s(c + 2)
+            if c + 1 < CHUNKS:
+                finish_factors(c + 1)
+            if c >= 0:
+                quantise(c)
+            if c + 2 < CHUNKS:
+                start_factors(c + 2)
             if c + 3 < CHUNKS:
-                load(c + 3)
-        quantise(CHUNKS - 1, 0)
-        quantise(CHUNKS - 1, 1)
-        multiply(CHUNKS - 1)
+                square(c + 3)
+            if c >= 0:
+                multiply(c, results)

@@ -44,11 +44,10 @@ def tile_capsulenetwork_pb_v_kernel(tc, p, Wr, s, grad_out, out):
         "n (c q x) -> c q n x", c=CHUNKS, q=P, x=BLOCKS * 16
     )
     halves = range(PASSES)
-    per_capsule = [P, PASSES * GROUPS]
 
     with ExitStack() as stack:
         const = stack.enter_context(tc.tile_pool(name="const", bufs=1))
-        stream = stack.enter_context(tc.tile_pool(name="stream", bufs=8))
+        stream = stack.enter_context(tc.tile_pool(name="stream", bufs=6))
         work = stack.enter_context(tc.tile_pool(name="work", bufs=2))
         small = stack.enter_context(tc.tile_pool(name="small", bufs=2))
         factor_banks = stack.enter_context(tc.psum_pool(name="factor_banks", bufs=2))
@@ -60,14 +59,11 @@ def tile_capsulenetwork_pb_v_kernel(tc, p, Wr, s, grad_out, out):
         squares_of = {}
         g_times_s_of = {}
         q_of = {}
-        root_of = {}
-        q_squared_of = {}
+        r_of = {}
+        w_of = {}
+        r_squared_of = {}
         d_of = {}
-        numerator_of = {}
-        z_of = {}
         factors_of = {}
-        a_g_of = {}
-        ds_of = {}
         grouped_of = {}
         codes_of = {}
         scales_of = {}
@@ -76,6 +72,10 @@ def tile_capsulenetwork_pb_v_kernel(tc, p, Wr, s, grad_out, out):
         make_identity(nc, identity[:])
         eps = const.tile([P, 1], F32)
         nc.vector.memset(eps[:], SQ_EPS)
+        one = const.tile([P, 1], F32)
+        nc.vector.memset(one[:], 1.0)
+        p_raw = const.tile([P, PASSES, PACK, NI], BF16)
+        p_grouped = const.tile([P, PASSES, NI, PACK], BF16, align_bytes=64)
         p_codes = const.tile([P, PASSES, NI], U32, align_bytes=64)
         p_scales = const.tile([P, PASSES, NI], U8, align_bytes=64)
 
@@ -88,6 +88,15 @@ def tile_capsulenetwork_pb_v_kernel(tc, p, Wr, s, grad_out, out):
                 nc.sync.dma_start(out=g_t[:], in_=g_rows[h, :, :, cols])
                 s_of[(c, h)] = s_t
                 g_of[(c, h)] = g_t
+
+        def quantise_p():
+            for h in halves:
+                nc.vector.tensor_copy(out=p_grouped[:, h], in_=p_raw[:, h].rearrange("q t w -> q w t"))
+            nc.vector.quantize_mx(
+                out=p_codes[:].rearrange("q h w -> q (h w)").bitcast(E4M3X4),
+                scales=p_scales[:].rearrange("q h w -> q (h w)"),
+                in_=p_grouped[:].rearrange("q h w t -> q (h w t)"),
+            )
 
         def square(c):
             for h in halves:
@@ -104,7 +113,7 @@ def tile_capsulenetwork_pb_v_kernel(tc, p, Wr, s, grad_out, out):
                 g_times_s_of[(c, h)] = g_times_s
 
         def sum_squares(c):
-            q = small.tile(per_capsule, F32)
+            q = small.tile([P, PASSES * GROUPS], F32)
             for h in halves:
                 nc.vector.tensor_reduce(
                     out=q[:, h * GROUPS : (h + 1) * GROUPS],
@@ -112,16 +121,21 @@ def tile_capsulenetwork_pb_v_kernel(tc, p, Wr, s, grad_out, out):
                     axis=AXIS_X,
                     op=ALU.add,
                 )
-            root = small.tile(per_capsule, F32)
-            nc.scalar.activation(out=root[:], in_=q[:], func=ACT.Sqrt, bias=eps[:, 0:1])
-            q_squared = small.tile(per_capsule, F32)
-            nc.scalar.activation(out=q_squared[:], in_=q[:], func=ACT.Square)
+            r = small.tile([P, PASSES * GROUPS], F32)
+            nc.scalar.activation(out=r[:], in_=q[:], func=ACT.Abs_reciprocal_sqrt, bias=eps[:, 0:1])
+            q1_squared = small.tile([P, PASSES * GROUPS], F32)
+            nc.scalar.activation(out=q1_squared[:], in_=q[:], func=ACT.Square, bias=one[:, 0:1])
+            w = small.tile([P, PASSES * GROUPS], F32)
+            nc.scalar.activation(out=w[:], in_=q1_squared[:], func=ACT.Abs_reciprocal_sqrt)
+            r_squared = small.tile([P, PASSES * GROUPS], F32)
+            nc.scalar.activation(out=r_squared[:], in_=r[:], func=ACT.Square)
             q_of[c] = q
-            root_of[c] = root
-            q_squared_of[c] = q_squared
+            r_of[c] = r
+            w_of[c] = w
+            r_squared_of[c] = r_squared
 
         def sum_products(c):
-            d = small.tile(per_capsule, F32)
+            d = small.tile([P, PASSES * GROUPS], F32)
             for h in halves:
                 nc.vector.tensor_reduce(
                     out=d[:, h * GROUPS : (h + 1) * GROUPS],
@@ -131,39 +145,23 @@ def tile_capsulenetwork_pb_v_kernel(tc, p, Wr, s, grad_out, out):
                 )
             d_of[c] = d
 
-
-        def start_factors(c):
+        def factors(c):
             q = q_of[c]
-            denominator = small.tile(per_capsule, F32)
-            nc.vector.scalar_tensor_tensor(
-                out=denominator[:], in0=q[:], scalar=1.0, in1=root_of[c][:], op0=ALU.add, op1=ALU.mult
-            )
-            numerator = small.tile(per_capsule, F32)
-            nc.vector.scalar_tensor_tensor(
-                out=numerator[:], in0=q[:], scalar=2.0 * SQ_EPS, in1=q_squared_of[c][:],
-                op0=ALU.add, op1=ALU.subtract,
-            )
-            z = small.tile(per_capsule, F32)
-            nc.vector.reciprocal(out=z[:], in_=denominator[:])
-            numerator_of[c] = numerator
-            z_of[c] = z
-
-        def finish_factors(c):
-            q = q_of[c]
-            z = z_of[c]
-            polynomial = small.tile(per_capsule, F32)
-            nc.vector.scalar_tensor_tensor(
-                out=polynomial[:], in0=q[:], scalar=1.0, in1=numerator_of[c][:], op0=ALU.add, op1=ALU.mult
-            )
-            z_d = small.tile(per_capsule, F32)
+            w = w_of[c]
+            width = [P, PASSES * GROUPS]
+            z = small.tile(width, F32)
+            nc.vector.tensor_tensor(out=z[:], in0=w[:], in1=r_of[c][:], op=ALU.mult)
+            q_r2 = small.tile(width, F32)
+            nc.vector.tensor_tensor(out=q_r2[:], in0=q[:], in1=r_squared_of[c][:], op=ALU.mult)
+            z_d = small.tile(width, F32)
             nc.vector.tensor_tensor(out=z_d[:], in0=z[:], in1=d_of[c][:], op=ALU.mult)
-            z_poly = small.tile(per_capsule, F32)
-            nc.vector.tensor_tensor(out=z_poly[:], in0=z[:], in1=polynomial[:], op=ALU.mult)
-            zz_d = small.tile(per_capsule, F32)
-            nc.vector.tensor_tensor(out=zz_d[:], in0=z[:], in1=z_d[:], op=ALU.mult)
+            bracket = small.tile(width, F32)
+            nc.vector.scalar_tensor_tensor(
+                out=bracket[:], in0=w[:], scalar=2.0, in1=q_r2[:], op0=ALU.mult, op1=ALU.subtract
+            )
             a_beta = small.tile([P, 2, PASSES * GROUPS], F32)
             nc.vector.tensor_tensor(out=a_beta[:, 0, :], in0=q[:], in1=z[:], op=ALU.mult)
-            nc.vector.tensor_tensor(out=a_beta[:, 1, :], in0=z_poly[:], in1=zz_d[:], op=ALU.mult)
+            nc.vector.tensor_tensor(out=a_beta[:, 1, :], in0=z_d[:], in1=bracket[:], op=ALU.mult)
             a_beta_psum = factor_banks.tile([P, 2, PASSES * GROUPS], F32)
             nc.tensor.matmul(
                 out=a_beta_psum[:].rearrange("q k x -> q (k x)"),
@@ -174,50 +172,46 @@ def tile_capsulenetwork_pb_v_kernel(tc, p, Wr, s, grad_out, out):
             )
             factors_of[c] = a_beta_psum
 
-        def scale(c, h):
-            groups = slice(h * GROUPS, (h + 1) * GROUPS)
-            a_g = work.tile([P, PACK, CHUNK], F32)
-            nc.vector.tensor_tensor(
-                out=by_capsule(a_g),
-                in0=by_capsule(g_of[(c, h)]),
-                in1=factors_of[c][:, 0, groups].unsqueeze(2).to_broadcast([P, GROUPS, CAP]),
-                op=ALU.mult,
-            )
-            nc.vector.tensor_tensor(
-                out=by_capsule(s_of[(c, h)]),
-                in0=by_capsule(s_of[(c, h)]),
-                in1=factors_of[c][:, 1, groups].unsqueeze(2).to_broadcast([P, GROUPS, CAP]),
-                op=ALU.mult,
-            )
-            a_g_of[(c, h)] = a_g
-
-        def add(c, h):
-            ds = work.tile([P, PACK, CHUNK], BF16)
-            nc.gpsimd.tensor_tensor(out=ds[:], in0=a_g_of[(c, h)][:], in1=s_of[(c, h)][:], op=ALU.add)
-            ds_of[(c, h)] = ds
-
-        def regroup(c, h):
-            ds_grouped = work.tile([P, CHUNK, PACK], BF16, align_bytes=64)
-            nc.scalar.copy(
-                out=ds_grouped[:].rearrange("q (m w) t -> q m w t", m=BLOCKS),
-                in_=ds_of[(c, h)][:].rearrange("q t (w m) -> q m w t", m=BLOCKS),
-            )
-            grouped_of[(c, h)] = ds_grouped
-
-        def quantise(c):
-            ds_codes = work.tile([P, PASSES, CHUNK], U32, align_bytes=64)
-            ds_scales = work.tile([P, PASSES, CHUNK], U8, align_bytes=64)
+        def scale_and_add(c):
             for h in halves:
-                nc.vector.quantize_mx(
-                    out=ds_codes[:, h, :].bitcast(E5M2X4),
-                    scales=ds_scales[:, h, :],
-                    in_=grouped_of[(c, h)][:].rearrange("q w t -> q (w t)"),
+                groups = slice(h * GROUPS, (h + 1) * GROUPS)
+                s_t = s_of[(c, h)]
+                a_g = work.tile([P, PACK, CHUNK], F32)
+                nc.vector.tensor_tensor(
+                    out=by_capsule(a_g),
+                    in0=by_capsule(g_of[(c, h)]),
+                    in1=factors_of[c][:, 0, groups].unsqueeze(2).to_broadcast([P, GROUPS, CAP]),
+                    op=ALU.mult,
                 )
-            codes_of[c] = ds_codes
-            scales_of[c] = ds_scales
+                nc.vector.tensor_tensor(
+                    out=by_capsule(s_t),
+                    in0=by_capsule(s_t),
+                    in1=factors_of[c][:, 1, groups].unsqueeze(2).to_broadcast([P, GROUPS, CAP]),
+                    op=ALU.mult,
+                )
+                ds = work.tile([P, PACK, CHUNK], BF16)
+                nc.gpsimd.tensor_tensor(out=ds[:], in0=a_g[:], in1=s_t[:], op=ALU.add)
+                ds_grouped = work.tile([P, CHUNK, PACK], BF16, align_bytes=64)
+                nc.scalar.copy(
+                    out=ds_grouped[:].rearrange("q (m w) t -> q m w t", m=BLOCKS),
+                    in_=ds[:].rearrange("q t (w m) -> q m w t", m=BLOCKS),
+                )
+                grouped_of[(c, h)] = ds_grouped
 
-        def multiply(c, results):
-            result = results.tile([P, 32, BLOCKS, 16], F32)
+        def quantise(c, h):
+            if h == 0:
+                ds_codes = work.tile([P, PASSES, CHUNK], U32, align_bytes=64)
+                ds_scales = work.tile([P, PASSES, CHUNK], U8, align_bytes=64)
+                codes_of[c] = ds_codes
+                scales_of[c] = ds_scales
+            nc.vector.quantize_mx(
+                out=codes_of[c][:, h, :].bitcast(E5M2X4),
+                scales=scales_of[c][:, h, :],
+                in_=grouped_of[(c, h)][:].rearrange("q w t -> q (w t)"),
+            )
+
+        def multiply(c):
+            result = work.tile([P, 32, BLOCKS, 16], F32)
             for m in range(BLOCKS):
                 block = slice(m * P, (m + 1) * P)
                 product = product_banks.tile([P, NI], F32)
@@ -239,49 +233,33 @@ def tile_capsulenetwork_pb_v_kernel(tc, p, Wr, s, grad_out, out):
             nc.sync.dma_start(out=out_chunks[c], in_=result[:].rearrange("q n m i -> q n (m i)"))
 
         load(0)
-        with tc.tile_pool(name="p_stage", bufs=1) as p_stage:
-            p_raw = p_stage.tile([P, PASSES, PACK, NI], BF16)
-            p_grouped = p_stage.tile([P, PASSES, NI, PACK], BF16, align_bytes=64)
-            for h in halves:
-                nc.sync.dma_start(out=p_raw[:, h], in_=p_rows[h])
-            load(1)
-            square(0)
-            sum_squares(0)
-            multiply_g_s(0)
-            for h in halves:
-                nc.vector.tensor_copy(out=p_grouped[:, h], in_=p_raw[:, h].rearrange("q t w -> q w t"))
-            nc.vector.quantize_mx(
-                out=p_codes[:].rearrange("q h w -> q (h w)").bitcast(E4M3X4),
-                scales=p_scales[:].rearrange("q h w -> q (h w)"),
-                in_=p_grouped[:].rearrange("q h w t -> q (h w t)"),
-            )
-        results = stack.enter_context(tc.tile_pool(name="results", bufs=2))
-        start_factors(0)
-        square(1)
+        for h in halves:
+            nc.sync.dma_start(out=p_raw[:, h], in_=p_rows[h])
+        load(1)
         load(2)
-
-        for c in range(-1, CHUNKS):
-            if c >= 0:
-                for h in halves:
-                    scale(c, h)
-                    add(c, h)
+        square(0)
+        multiply_g_s(0)
+        sum_squares(0)
+        square(1)
+        for c in range(CHUNKS):
+            sum_products(c)
             if c + 1 < CHUNKS:
-                sum_products(c + 1)
-            if c + 4 < CHUNKS:
-                load(c + 4)
-            if c >= 0:
-                for h in halves:
-                    regroup(c, h)
-            if c + 2 < CHUNKS:
-                sum_squares(c + 2)
-                multiply_g_s(c + 2)
+                multiply_g_s(c + 1)
+            if c >= 1:
+                quantise(c - 1, 0)
+            factors(c)
+            if c == 0:
+                quantise_p()
+            if c >= 1:
+                quantise(c - 1, 1)
+                multiply(c - 1)
             if c + 1 < CHUNKS:
-                finish_factors(c + 1)
-            if c >= 0:
-                quantise(c)
+                sum_squares(c + 1)
             if c + 2 < CHUNKS:
-                start_factors(c + 2)
+                square(c + 2)
+            scale_and_add(c)
             if c + 3 < CHUNKS:
-                square(c + 3)
-            if c >= 0:
-                multiply(c, results)
+                load(c + 3)
+        quantise(CHUNKS - 1, 0)
+        quantise(CHUNKS - 1, 1)
+        multiply(CHUNKS - 1)

@@ -191,24 +191,24 @@ def tile_capsulenetwork_pb_v_kernel(tc, p, Wr, s, grad_out, out):
                 )
                 ds = work.tile([P, PACK, CHUNK], BF16)
                 nc.gpsimd.tensor_tensor(out=ds[:], in0=a_g[:], in1=s_t[:], op=ALU.add)
-                ds_grouped = work.tile([P, CHUNK, PACK], BF16, align_bytes=64)
+                ds_grouped = work.tile([P, CHUNK, PACK], BF16, align_bytes=64, bufs=2 * PASSES)
                 nc.scalar.copy(
                     out=ds_grouped[:].rearrange("q (m w) t -> q m w t", m=BLOCKS),
                     in_=ds[:].rearrange("q t (w m) -> q m w t", m=BLOCKS),
                 )
                 grouped_of[(c, h)] = ds_grouped
 
-        def quantise(c, h):
-            if h == 0:
-                ds_codes = work.tile([P, PASSES, CHUNK], U32, align_bytes=64)
-                ds_scales = work.tile([P, PASSES, CHUNK], U8, align_bytes=64)
-                codes_of[c] = ds_codes
-                scales_of[c] = ds_scales
-            nc.vector.quantize_mx(
-                out=codes_of[c][:, h, :].bitcast(E5M2X4),
-                scales=scales_of[c][:, h, :],
-                in_=grouped_of[(c, h)][:].rearrange("q w t -> q (w t)"),
-            )
+        def quantise(c):
+            ds_codes = work.tile([P, PASSES, CHUNK], U32, align_bytes=64)
+            ds_scales = work.tile([P, PASSES, CHUNK], U8, align_bytes=64)
+            for h in halves:
+                nc.vector.quantize_mx(
+                    out=ds_codes[:, h, :].bitcast(E5M2X4),
+                    scales=ds_scales[:, h, :],
+                    in_=grouped_of[(c, h)][:].rearrange("q w t -> q (w t)"),
+                )
+            codes_of[c] = ds_codes
+            scales_of[c] = ds_scales
 
         def multiply(c):
             result = work.tile([P, 32, BLOCKS, 16], F32)
@@ -245,14 +245,13 @@ def tile_capsulenetwork_pb_v_kernel(tc, p, Wr, s, grad_out, out):
             sum_products(c)
             if c + 1 < CHUNKS:
                 multiply_g_s(c + 1)
-            if c >= 1:
-                quantise(c - 1, 0)
+            if c >= 2:
+                quantise(c - 2)
             factors(c)
             if c == 0:
                 quantise_p()
-            if c >= 1:
-                quantise(c - 1, 1)
-                multiply(c - 1)
+            if c >= 2:
+                multiply(c - 2)
             if c + 1 < CHUNKS:
                 sum_squares(c + 1)
             if c + 2 < CHUNKS:
@@ -260,6 +259,6 @@ def tile_capsulenetwork_pb_v_kernel(tc, p, Wr, s, grad_out, out):
             scale_and_add(c)
             if c + 3 < CHUNKS:
                 load(c + 3)
-        quantise(CHUNKS - 1, 0)
-        quantise(CHUNKS - 1, 1)
-        multiply(CHUNKS - 1)
+        for c in (CHUNKS - 2, CHUNKS - 1):
+            quantise(c)
+            multiply(c)

@@ -61,7 +61,7 @@ def tile_capsulenetwork_pb_v_kernel(tc, p, Wr, s, grad_out, out):
         q_of = {}
         r_of = {}
         w_of = {}
-        r_squared_of = {}
+        q_r2_of = {}
         d_of = {}
         factors_of = {}
         grouped_of = {}
@@ -89,9 +89,11 @@ def tile_capsulenetwork_pb_v_kernel(tc, p, Wr, s, grad_out, out):
                 s_of[(c, h)] = s_t
                 g_of[(c, h)] = g_t
 
-        def quantise_p():
+        def regroup_p():
             for h in halves:
-                nc.vector.tensor_copy(out=p_grouped[:, h], in_=p_raw[:, h].rearrange("q t w -> q w t"))
+                nc.scalar.copy(out=p_grouped[:, h], in_=p_raw[:, h].rearrange("q t w -> q w t"))
+
+        def quantise_p():
             nc.vector.quantize_mx(
                 out=p_codes[:].rearrange("q h w -> q (h w)").bitcast(E4M3X4),
                 scales=p_scales[:].rearrange("q h w -> q (h w)"),
@@ -129,10 +131,14 @@ def tile_capsulenetwork_pb_v_kernel(tc, p, Wr, s, grad_out, out):
             nc.scalar.activation(out=w[:], in_=q1_squared[:], func=ACT.Abs_reciprocal_sqrt)
             r_squared = small.tile([P, PASSES * GROUPS], F32)
             nc.scalar.activation(out=r_squared[:], in_=r[:], func=ACT.Square)
+            q_r2 = small.tile([P, PASSES * GROUPS], F32)
+            nc.scalar.activation(
+                out=q_r2[:], in_=r_squared[:], func=ACT.Identity, scale=-SQ_EPS, bias=one[:, 0:1]
+            )
             q_of[c] = q
             r_of[c] = r
             w_of[c] = w
-            r_squared_of[c] = r_squared
+            q_r2_of[c] = q_r2
 
         def sum_products(c):
             d = small.tile([P, PASSES * GROUPS], F32)
@@ -151,14 +157,12 @@ def tile_capsulenetwork_pb_v_kernel(tc, p, Wr, s, grad_out, out):
             width = [P, PASSES * GROUPS]
             z = small.tile(width, F32)
             nc.vector.tensor_tensor(out=z[:], in0=w[:], in1=r_of[c][:], op=ALU.mult)
-            q_r2 = small.tile(width, F32)
-            nc.vector.tensor_tensor(out=q_r2[:], in0=q[:], in1=r_squared_of[c][:], op=ALU.mult)
-            z_d = small.tile(width, F32)
-            nc.vector.tensor_tensor(out=z_d[:], in0=z[:], in1=d_of[c][:], op=ALU.mult)
             bracket = small.tile(width, F32)
             nc.vector.scalar_tensor_tensor(
-                out=bracket[:], in0=w[:], scalar=2.0, in1=q_r2[:], op0=ALU.mult, op1=ALU.subtract
+                out=bracket[:], in0=w[:], scalar=2.0, in1=q_r2_of[c][:], op0=ALU.mult, op1=ALU.subtract
             )
+            z_d = small.tile(width, F32)
+            nc.vector.tensor_tensor(out=z_d[:], in0=z[:], in1=d_of[c][:], op=ALU.mult)
             a_beta = small.tile([P, 2, PASSES * GROUPS], F32)
             nc.vector.tensor_tensor(out=a_beta[:, 0, :], in0=q[:], in1=z[:], op=ALU.mult)
             nc.vector.tensor_tensor(out=a_beta[:, 1, :], in0=z_d[:], in1=bracket[:], op=ALU.mult)
@@ -190,7 +194,8 @@ def tile_capsulenetwork_pb_v_kernel(tc, p, Wr, s, grad_out, out):
                     op=ALU.mult,
                 )
                 ds = work.tile([P, PACK, CHUNK], BF16)
-                nc.gpsimd.tensor_tensor(out=ds[:], in0=a_g[:], in1=s_t[:], op=ALU.add)
+                adder = nc.vector if (c, h) == (CHUNKS - 1, PASSES - 1) else nc.gpsimd
+                adder.tensor_tensor(out=ds[:], in0=a_g[:], in1=s_t[:], op=ALU.add)
                 ds_grouped = work.tile([P, CHUNK, PACK], BF16, align_bytes=64, bufs=2 * PASSES)
                 nc.scalar.copy(
                     out=ds_grouped[:].rearrange("q (m w) t -> q m w t", m=BLOCKS),
@@ -240,6 +245,7 @@ def tile_capsulenetwork_pb_v_kernel(tc, p, Wr, s, grad_out, out):
         square(0)
         multiply_g_s(0)
         sum_squares(0)
+        regroup_p()
         square(1)
         for c in range(CHUNKS):
             sum_products(c)

@@ -193,14 +193,21 @@ def tile_capsulenetwork_pb_v_kernel(tc, p, Wr, s, grad_out, out):
                     in1=factors_of[c][:, 1, groups].unsqueeze(2).to_broadcast([P, GROUPS, CAP]),
                     op=ALU.mult,
                 )
-                ds = work.tile([P, PACK, CHUNK], BF16)
-                adder = nc.vector if (c, h) == (CHUNKS - 1, PASSES - 1) else nc.gpsimd
-                adder.tensor_tensor(out=ds[:], in0=a_g[:], in1=s_t[:], op=ALU.add)
                 ds_grouped = work.tile([P, CHUNK, PACK], BF16, align_bytes=64, bufs=2 * PASSES)
-                nc.scalar.copy(
-                    out=ds_grouped[:].rearrange("q (m w) t -> q m w t", m=BLOCKS),
-                    in_=ds[:].rearrange("q t (w m) -> q m w t", m=BLOCKS),
-                )
+                if (c, h) == (CHUNKS - 1, PASSES - 1):
+                    nc.vector.tensor_tensor(
+                        out=ds_grouped[:].rearrange("q (m w) t -> q m w t", m=BLOCKS),
+                        in0=a_g[:].rearrange("q t (w m) -> q m w t", m=BLOCKS),
+                        in1=s_t[:].rearrange("q t (w m) -> q m w t", m=BLOCKS),
+                        op=ALU.add,
+                    )
+                else:
+                    ds = work.tile([P, PACK, CHUNK], BF16)
+                    nc.gpsimd.tensor_tensor(out=ds[:], in0=a_g[:], in1=s_t[:], op=ALU.add)
+                    nc.scalar.copy(
+                        out=ds_grouped[:].rearrange("q (m w) t -> q m w t", m=BLOCKS),
+                        in_=ds[:].rearrange("q t (w m) -> q m w t", m=BLOCKS),
+                    )
                 grouped_of[(c, h)] = ds_grouped
 
         def quantise(c):
@@ -230,22 +237,28 @@ def tile_capsulenetwork_pb_v_kernel(tc, p, Wr, s, grad_out, out):
                         start=(h == 0),
                         stop=(h == PASSES - 1),
                     )
-                nc.scalar.mul(
-                    out=result[:, :, m, :],
-                    in_=product[:].rearrange("q (n i) -> q n i", i=16),
-                    mul=COUPLING,
-                )
+                if c == CHUNKS - 1 and m % 2 == 1:
+                    nc.vector.tensor_scalar_mul(
+                        out=result[:, :, m, :],
+                        in0=product[:].rearrange("q (n i) -> q n i", i=16),
+                        scalar1=COUPLING,
+                    )
+                else:
+                    nc.scalar.mul(
+                        out=result[:, :, m, :],
+                        in_=product[:].rearrange("q (n i) -> q n i", i=16),
+                        mul=COUPLING,
+                    )
             nc.sync.dma_start(out=out_chunks[c], in_=result[:].rearrange("q n m i -> q n (m i)"))
 
         load(0)
+        load(1)
         for h in halves:
             nc.sync.dma_start(out=p_raw[:, h], in_=p_rows[h])
-        load(1)
         load(2)
         square(0)
         multiply_g_s(0)
         sum_squares(0)
-        regroup_p()
         square(1)
         for c in range(CHUNKS):
             sum_products(c)
@@ -254,17 +267,21 @@ def tile_capsulenetwork_pb_v_kernel(tc, p, Wr, s, grad_out, out):
             if c >= 2:
                 quantise(c - 2)
             factors(c)
-            if c == 0:
+            if c == 1:
                 quantise_p()
             if c >= 2:
                 multiply(c - 2)
+            if c == CHUNKS - 1:
+                quantise(c - 1)
+                multiply(c - 1)
             if c + 1 < CHUNKS:
                 sum_squares(c + 1)
             if c + 2 < CHUNKS:
                 square(c + 2)
+            if c == 0:
+                regroup_p()
             scale_and_add(c)
             if c + 3 < CHUNKS:
                 load(c + 3)
-        for c in (CHUNKS - 2, CHUNKS - 1):
-            quantise(c)
-            multiply(c)
+        quantise(CHUNKS - 1)
+        multiply(CHUNKS - 1)

@@ -24,6 +24,7 @@ CHUNK = 512
 CHUNKS = COLS // CHUNK
 BLOCKS = CHUNK // P
 GROUPS = PACK * (CHUNK // CAP)
+GPSIMD_COLS = 384
 SQ_EPS = 1e-8
 COUPLING = 1.0 / 256.0
 
@@ -52,6 +53,7 @@ def tile_capsulenetwork_pb_v_kernel(tc, p, Wr, s, grad_out, out):
         small = stack.enter_context(tc.tile_pool(name="small", bufs=2))
         factor_banks = stack.enter_context(tc.psum_pool(name="factor_banks", bufs=2))
         product_banks = stack.enter_context(tc.psum_pool(name="product_banks", bufs=4))
+        sum_banks = stack.enter_context(tc.psum_pool(name="sum_banks", bufs=2))
         stack.enter_context(tc.manual_schedule())
 
         s_of = {}
@@ -200,6 +202,30 @@ def tile_capsulenetwork_pb_v_kernel(tc, p, Wr, s, grad_out, out):
                         in0=a_g[:].rearrange("q t (w m) -> q m w t", m=BLOCKS),
                         in1=s_t[:].rearrange("q t (w m) -> q m w t", m=BLOCKS),
                         op=ALU.add,
+                    )
+                elif h == 0:
+                    grouped = ds_grouped[:].rearrange("q (m w) t -> q m w t", m=BLOCKS)
+                    ds = work.tile([P, PACK, CHUNK], BF16)
+                    nc.gpsimd.tensor_tensor(
+                        out=ds[:, :, 0:GPSIMD_COLS],
+                        in0=a_g[:, :, 0:GPSIMD_COLS],
+                        in1=s_t[:, :, 0:GPSIMD_COLS],
+                        op=ALU.add,
+                    )
+                    rest = sum_banks.tile([P, PACK, CHUNK - GPSIMD_COLS], F32)
+                    nc.tensor.matmul(
+                        out=rest[:], lhsT=identity[:], rhs=a_g[:, :, GPSIMD_COLS:CHUNK], start=True, stop=False
+                    )
+                    nc.tensor.matmul(
+                        out=rest[:], lhsT=identity[:], rhs=s_t[:, :, GPSIMD_COLS:CHUNK], start=False, stop=True
+                    )
+                    nc.scalar.copy(
+                        out=grouped[:, :, 0 : GPSIMD_COLS // BLOCKS, :],
+                        in_=ds[:, :, 0:GPSIMD_COLS].rearrange("q t (w m) -> q m w t", m=BLOCKS),
+                    )
+                    nc.scalar.copy(
+                        out=grouped[:, :, GPSIMD_COLS // BLOCKS : P, :],
+                        in_=rest[:].rearrange("q t (w m) -> q m w t", m=BLOCKS),
                     )
                 else:
                     ds = work.tile([P, PACK, CHUNK], BF16)

@@ -23,6 +23,8 @@ COLS = 256 * CAP
 CHUNK = 512
 CHUNKS = COLS // CHUNK
 BLOCKS = CHUNK // P
+CAPSULES = CHUNK // CAP
+SCALAR_ROWS = 2
 GROUPS = PACK * (CHUNK // CAP)
 GPSIMD_COLS = 384
 SQ_EPS = 1e-8
@@ -66,6 +68,7 @@ def tile_capsulenetwork_pb_v_kernel(tc, p, Wr, s, grad_out, out):
         q_r2_of = {}
         d_of = {}
         factors_of = {}
+        a_beta_of = {}
         grouped_of = {}
         codes_of = {}
         scales_of = {}
@@ -177,6 +180,18 @@ def tile_capsulenetwork_pb_v_kernel(tc, p, Wr, s, grad_out, out):
                 stop=True,
             )
             factors_of[c] = a_beta_psum
+            a_beta_of[c] = a_beta
+
+        def scale_s_on_scalar(c):
+            h = PASSES - 1
+            s_t = s_of[(c, h)]
+            for t in range(PACK - SCALAR_ROWS, PACK):
+                for j in range(CAPSULES):
+                    group = h * GROUPS + t * CAPSULES + j
+                    values = s_t[:, t, j * CAP : (j + 1) * CAP]
+                    nc.scalar.activation(
+                        out=values, in_=values, func=ACT.Copy, scale=a_beta_of[c][:, 1, group : group + 1]
+                    )
 
         def scale_and_add(c):
             for h in halves:
@@ -189,10 +204,14 @@ def tile_capsulenetwork_pb_v_kernel(tc, p, Wr, s, grad_out, out):
                     in1=factors_of[c][:, 0, groups].unsqueeze(2).to_broadcast([P, GROUPS, CAP]),
                     op=ALU.mult,
                 )
+                rows = PACK - SCALAR_ROWS if (h == PASSES - 1 and c < CHUNKS - 1) else PACK
+                mine = s_t[:, 0:rows, :].rearrange("q t (j o) -> q (t j) o", o=CAP)
                 nc.vector.tensor_tensor(
-                    out=by_capsule(s_t),
-                    in0=by_capsule(s_t),
-                    in1=factors_of[c][:, 1, groups].unsqueeze(2).to_broadcast([P, GROUPS, CAP]),
+                    out=mine,
+                    in0=mine,
+                    in1=factors_of[c][:, 1, h * GROUPS : h * GROUPS + rows * CAPSULES]
+                    .unsqueeze(2)
+                    .to_broadcast([P, rows * CAPSULES, CAP]),
                     op=ALU.mult,
                 )
                 ds_grouped = work.tile([P, CHUNK, PACK], BF16, align_bytes=64, bufs=2 * PASSES)
@@ -300,6 +319,8 @@ def tile_capsulenetwork_pb_v_kernel(tc, p, Wr, s, grad_out, out):
             if c == CHUNKS - 1:
                 quantise(c - 1)
                 multiply(c - 1)
+            if c < CHUNKS - 1:
+                scale_s_on_scalar(c)
             if c + 1 < CHUNKS:
                 sum_squares(c + 1)
             if c + 2 < CHUNKS:

@@ -17,7 +17,8 @@ P = 128
 PACK = 4
 BATCH = 1024
 PASSES = BATCH // (P * PACK)
-NI = 32 * 16
+PRIMARY = 32
+NI = PRIMARY * 16
 CAP = 16
 COLS = 256 * CAP
 CHUNK = 512
@@ -84,13 +85,18 @@ def tile_capsulenetwork_pb_v_kernel(tc, p, Wr, s, grad_out, out):
         p_codes = const.tile([P, PASSES, NI], U32, align_bytes=64)
         p_scales = const.tile([P, PASSES, NI], U8, align_bytes=64)
 
+        def pieces(c, h):
+            step = PACK // 2 if (c, h) == (0, 0) else PACK
+            return [slice(t, t + step) for t in range(0, PACK, step)]
+
         def load(c):
             cols = slice(c * CHUNK, (c + 1) * CHUNK)
             for h in halves:
                 s_t = stream.tile([P, PACK, CHUNK], F32)
-                nc.sync.dma_start(out=s_t[:], in_=s_rows[h, :, :, cols])
                 g_t = stream.tile([P, PACK, CHUNK], BF16)
-                nc.sync.dma_start(out=g_t[:], in_=g_rows[h, :, :, cols])
+                for rows in pieces(c, h):
+                    nc.sync.dma_start(out=s_t[:, rows, :], in_=s_rows[h, :, rows, cols])
+                    nc.sync.dma_start(out=g_t[:, rows, :], in_=g_rows[h, :, rows, cols])
                 s_of[(c, h)] = s_t
                 g_of[(c, h)] = g_t
 
@@ -108,26 +114,32 @@ def tile_capsulenetwork_pb_v_kernel(tc, p, Wr, s, grad_out, out):
         def square(c):
             for h in halves:
                 squares = work.tile([P, PACK, CHUNK], F32)
-                nc.scalar.activation(out=squares[:], in_=s_of[(c, h)][:], func=ACT.Square)
+                for rows in pieces(c, h):
+                    nc.scalar.activation(out=squares[:, rows, :], in_=s_of[(c, h)][:, rows, :], func=ACT.Square)
                 squares_of[(c, h)] = squares
 
         def multiply_g_s(c):
             for h in halves:
                 g_times_s = work.tile([P, PACK, CHUNK], F32)
-                nc.gpsimd.tensor_tensor(
-                    out=g_times_s[:], in0=g_of[(c, h)][:], in1=s_of[(c, h)][:], op=ALU.mult
-                )
+                for rows in pieces(c, h):
+                    nc.gpsimd.tensor_tensor(
+                        out=g_times_s[:, rows, :],
+                        in0=g_of[(c, h)][:, rows, :],
+                        in1=s_of[(c, h)][:, rows, :],
+                        op=ALU.mult,
+                    )
                 g_times_s_of[(c, h)] = g_times_s
 
         def sum_squares(c):
             q = small.tile([P, PASSES * GROUPS], F32)
             for h in halves:
-                nc.vector.tensor_reduce(
-                    out=q[:, h * GROUPS : (h + 1) * GROUPS],
-                    in_=by_capsule(squares_of[(c, h)]),
-                    axis=AXIS_X,
-                    op=ALU.add,
-                )
+                for rows in pieces(c, h):
+                    nc.vector.tensor_reduce(
+                        out=q[:, h * GROUPS + rows.start * CAPSULES : h * GROUPS + rows.stop * CAPSULES],
+                        in_=squares_of[(c, h)][:, rows, :].rearrange("q t (j o) -> q (t j) o", o=CAP),
+                        axis=AXIS_X,
+                        op=ALU.add,
+                    )
             r = small.tile([P, PASSES * GROUPS], F32)
             nc.scalar.activation(out=r[:], in_=q[:], func=ACT.Abs_reciprocal_sqrt, bias=eps[:, 0:1])
             q1_squared = small.tile([P, PASSES * GROUPS], F32)
@@ -197,11 +209,12 @@ def tile_capsulenetwork_pb_v_kernel(tc, p, Wr, s, grad_out, out):
             for h in halves:
                 groups = slice(h * GROUPS, (h + 1) * GROUPS)
                 s_t = s_of[(c, h)]
+                a_beta = a_beta_of[c] if (c == CHUNKS - 1 and h == 0) else factors_of[c]
                 a_g = work.tile([P, PACK, CHUNK], F32)
                 nc.vector.tensor_tensor(
                     out=by_capsule(a_g),
                     in0=by_capsule(g_of[(c, h)]),
-                    in1=factors_of[c][:, 0, groups].unsqueeze(2).to_broadcast([P, GROUPS, CAP]),
+                    in1=a_beta[:, 0, groups].unsqueeze(2).to_broadcast([P, GROUPS, CAP]),
                     op=ALU.mult,
                 )
                 rows = PACK - SCALAR_ROWS if (h == PASSES - 1 and c < CHUNKS - 1) else PACK
@@ -209,13 +222,15 @@ def tile_capsulenetwork_pb_v_kernel(tc, p, Wr, s, grad_out, out):
                 nc.vector.tensor_tensor(
                     out=mine,
                     in0=mine,
-                    in1=factors_of[c][:, 1, h * GROUPS : h * GROUPS + rows * CAPSULES]
+                    in1=a_beta[:, 1, h * GROUPS : h * GROUPS + rows * CAPSULES]
                     .unsqueeze(2)
                     .to_broadcast([P, rows * CAPSULES, CAP]),
                     op=ALU.mult,
                 )
                 ds_grouped = work.tile([P, CHUNK, PACK], BF16, align_bytes=64, bufs=2 * PASSES)
                 if (c, h) == (CHUNKS - 1, PASSES - 1):
+                    quantise(c - 1)
+                    multiply(c - 1)
                     nc.vector.tensor_tensor(
                         out=ds_grouped[:].rearrange("q (m w) t -> q m w t", m=BLOCKS),
                         in0=a_g[:].rearrange("q t (w m) -> q m w t", m=BLOCKS),
@@ -268,13 +283,16 @@ def tile_capsulenetwork_pb_v_kernel(tc, p, Wr, s, grad_out, out):
             scales_of[c] = ds_scales
 
         def multiply(c):
-            result = work.tile([P, 32, BLOCKS, 16], F32)
+            result = work.tile([P, PRIMARY, BLOCKS, 16], F32)
+            products = []
             for m in range(BLOCKS):
-                block = slice(m * P, (m + 1) * P)
                 product = product_banks.tile([P, NI], F32)
-                for h in halves:
+                products.append(product)
+            for h in halves:
+                for m in range(BLOCKS):
+                    block = slice(m * P, (m + 1) * P)
                     nc.tensor.matmul_mx(
-                        out=product[:],
+                        out=products[m][:],
                         lhsT=codes_of[c][:, h, block].bitcast(E5M2X4),
                         lhsT_scale=scales_of[c][:, h, block],
                         rhs=p_codes[:, h, :].bitcast(E4M3X4),
@@ -282,19 +300,21 @@ def tile_capsulenetwork_pb_v_kernel(tc, p, Wr, s, grad_out, out):
                         start=(h == 0),
                         stop=(h == PASSES - 1),
                     )
-                if c == CHUNKS - 1 and m % 2 == 1:
-                    nc.vector.tensor_scalar_mul(
-                        out=result[:, :, m, :],
-                        in0=product[:].rearrange("q (n i) -> q n i", i=16),
-                        scalar1=COUPLING,
-                    )
-                else:
-                    nc.scalar.mul(
-                        out=result[:, :, m, :],
-                        in_=product[:].rearrange("q (n i) -> q n i", i=16),
-                        mul=COUPLING,
-                    )
-            nc.sync.dma_start(out=out_chunks[c], in_=result[:].rearrange("q n m i -> q n (m i)"))
+            last = c == CHUNKS - 1
+            stores = 2 if last else 1
+            share = PRIMARY // stores
+            for k in range(stores):
+                capsules = slice(k * share, (k + 1) * share)
+                for m in range(BLOCKS):
+                    part = products[m][:].rearrange("q (n i) -> q n i", i=16)[:, capsules, :]
+                    if last and m % 2 == 1:
+                        nc.vector.tensor_scalar_mul(out=result[:, capsules, m, :], in0=part, scalar1=COUPLING)
+                    else:
+                        nc.scalar.mul(out=result[:, capsules, m, :], in_=part, mul=COUPLING)
+                nc.sync.dma_start(
+                    out=out_chunks[c][:, capsules, :],
+                    in_=result[:, capsules, :, :].rearrange("q n m i -> q n (m i)"),
+                )
 
         load(0)
         load(1)
@@ -316,9 +336,6 @@ def tile_capsulenetwork_pb_v_kernel(tc, p, Wr, s, grad_out, out):
                 quantise_p()
             if c >= 2:
                 multiply(c - 2)
-            if c == CHUNKS - 1:
-                quantise(c - 1)
-                multiply(c - 1)
             if c < CHUNKS - 1:
                 scale_s_on_scalar(c)
             if c + 1 < CHUNKS:

@@ -25,7 +25,7 @@ CHUNK = 512
 CHUNKS = COLS // CHUNK
 BLOCKS = CHUNK // P
 CAPSULES = CHUNK // CAP
-SCALAR_ROWS = 2
+SCALAR_ROWS = 3
 GROUPS = PACK * (CHUNK // CAP)
 GPSIMD_COLS = 384
 SQ_EPS = 1e-8

@@ -239,11 +239,10 @@ def tile_capsulenetwork_pb_v_kernel(tc, p, Wr, s, grad_out, out):
                     )
                 elif h == 0:
                     grouped = ds_grouped[:].rearrange("q (m w) t -> q m w t", m=BLOCKS)
-                    ds = work.tile([P, PACK, CHUNK], BF16)
                     nc.gpsimd.tensor_tensor(
-                        out=ds[:, :, 0:GPSIMD_COLS],
-                        in0=a_g[:, :, 0:GPSIMD_COLS],
-                        in1=s_t[:, :, 0:GPSIMD_COLS],
+                        out=ds_grouped[:].rearrange("q (m w) t -> q w t m", m=BLOCKS)[:, 0 : GPSIMD_COLS // BLOCKS],
+                        in0=a_g[:, :, 0:GPSIMD_COLS].rearrange("q t (w m) -> q w t m", m=BLOCKS),
+                        in1=s_t[:, :, 0:GPSIMD_COLS].rearrange("q t (w m) -> q w t m", m=BLOCKS),
                         op=ALU.add,
                     )
                     rest = sum_banks.tile([P, PACK, CHUNK - GPSIMD_COLS], F32)
@@ -254,19 +253,15 @@ def tile_capsulenetwork_pb_v_kernel(tc, p, Wr, s, grad_out, out):
                         out=rest[:], lhsT=identity[:], rhs=s_t[:, :, GPSIMD_COLS:CHUNK], start=False, stop=True
                     )
                     nc.scalar.copy(
-                        out=grouped[:, :, 0 : GPSIMD_COLS // BLOCKS, :],
-                        in_=ds[:, :, 0:GPSIMD_COLS].rearrange("q t (w m) -> q m w t", m=BLOCKS),
-                    )
-                    nc.scalar.copy(
                         out=grouped[:, :, GPSIMD_COLS // BLOCKS : P, :],
                         in_=rest[:].rearrange("q t (w m) -> q m w t", m=BLOCKS),
                     )
                 else:
-                    ds = work.tile([P, PACK, CHUNK], BF16)
-                    nc.gpsimd.tensor_tensor(out=ds[:], in0=a_g[:], in1=s_t[:], op=ALU.add)
-                    nc.scalar.copy(
-                        out=ds_grouped[:].rearrange("q (m w) t -> q m w t", m=BLOCKS),
-                        in_=ds[:].rearrange("q t (w m) -> q m w t", m=BLOCKS),
+                    nc.gpsimd.tensor_tensor(
+                        out=ds_grouped[:].rearrange("q (m w) t -> q w t m", m=BLOCKS),
+                        in0=a_g[:].rearrange("q t (w m) -> q w t m", m=BLOCKS),
+                        in1=s_t[:].rearrange("q t (w m) -> q w t m", m=BLOCKS),
+                        op=ALU.add,
                     )
                 grouped_of[(c, h)] = ds_grouped
 

@@ -25,7 +25,7 @@ CHUNK = 512
 CHUNKS = COLS // CHUNK
 BLOCKS = CHUNK // P
 CAPSULES = CHUNK // CAP
-SCALAR_ROWS = 3
+SCALAR_ROWS = (2, 4)
 GROUPS = PACK * (CHUNK // CAP)
 GPSIMD_COLS = 384
 SQ_EPS = 1e-8
@@ -111,35 +111,38 @@ def tile_capsulenetwork_pb_v_kernel(tc, p, Wr, s, grad_out, out):
                 in_=p_grouped[:].rearrange("q h w t -> q (h w t)"),
             )
 
-        def square(c):
-            for h in halves:
-                squares = work.tile([P, PACK, CHUNK], F32)
-                for rows in pieces(c, h):
-                    nc.scalar.activation(out=squares[:, rows, :], in_=s_of[(c, h)][:, rows, :], func=ACT.Square)
-                squares_of[(c, h)] = squares
+        def square(c, h):
+            squares = work.tile([P, PACK, CHUNK], F32)
+            for rows in pieces(c, h):
+                nc.scalar.activation(out=squares[:, rows, :], in_=s_of[(c, h)][:, rows, :], func=ACT.Square)
+            squares_of[(c, h)] = squares
 
-        def multiply_g_s(c):
-            for h in halves:
-                g_times_s = work.tile([P, PACK, CHUNK], F32)
-                for rows in pieces(c, h):
-                    nc.gpsimd.tensor_tensor(
-                        out=g_times_s[:, rows, :],
-                        in0=g_of[(c, h)][:, rows, :],
-                        in1=s_of[(c, h)][:, rows, :],
-                        op=ALU.mult,
-                    )
-                g_times_s_of[(c, h)] = g_times_s
+        def multiply_g_s(c, h, engine):
+            g_times_s = work.tile([P, PACK, CHUNK], F32)
+            for rows in pieces(c, h):
+                engine.tensor_tensor(
+                    out=g_times_s[:, rows, :],
+                    in0=g_of[(c, h)][:, rows, :],
+                    in1=s_of[(c, h)][:, rows, :],
+                    op=ALU.mult,
+                )
+            g_times_s_of[(c, h)] = g_times_s
 
-        def sum_squares(c):
-            q = small.tile([P, PASSES * GROUPS], F32)
-            for h in halves:
-                for rows in pieces(c, h):
-                    nc.vector.tensor_reduce(
-                        out=q[:, h * GROUPS + rows.start * CAPSULES : h * GROUPS + rows.stop * CAPSULES],
-                        in_=squares_of[(c, h)][:, rows, :].rearrange("q t (j o) -> q (t j) o", o=CAP),
-                        axis=AXIS_X,
-                        op=ALU.add,
-                    )
+        def sum_squares(c, h):
+            if h == 0:
+                q = small.tile([P, PASSES * GROUPS], F32)
+                q_of[c] = q
+            q = q_of[c]
+            for rows in pieces(c, h):
+                nc.vector.tensor_reduce(
+                    out=q[:, h * GROUPS + rows.start * CAPSULES : h * GROUPS + rows.stop * CAPSULES],
+                    in_=squares_of[(c, h)][:, rows, :].rearrange("q t (j o) -> q (t j) o", o=CAP),
+                    axis=AXIS_X,
+                    op=ALU.add,
+                )
+
+        def functions_of_q(c):
+            q = q_of[c]
             r = small.tile([P, PASSES * GROUPS], F32)
             nc.scalar.activation(out=r[:], in_=q[:], func=ACT.Abs_reciprocal_sqrt, bias=eps[:, 0:1])
             q1_squared = small.tile([P, PASSES * GROUPS], F32)
@@ -152,21 +155,21 @@ def tile_capsulenetwork_pb_v_kernel(tc, p, Wr, s, grad_out, out):
             nc.scalar.activation(
                 out=q_r2[:], in_=r_squared[:], func=ACT.Identity, scale=-SQ_EPS, bias=one[:, 0:1]
             )
-            q_of[c] = q
             r_of[c] = r
             w_of[c] = w
             q_r2_of[c] = q_r2
 
-        def sum_products(c):
-            d = small.tile([P, PASSES * GROUPS], F32)
-            for h in halves:
-                nc.vector.tensor_reduce(
-                    out=d[:, h * GROUPS : (h + 1) * GROUPS],
-                    in_=by_capsule(g_times_s_of[(c, h)]),
-                    axis=AXIS_X,
-                    op=ALU.add,
-                )
-            d_of[c] = d
+        def sum_products(c, h):
+            if c not in d_of:
+                d = small.tile([P, PASSES * GROUPS], F32)
+                d_of[c] = d
+            d = d_of[c]
+            nc.vector.tensor_reduce(
+                out=d[:, h * GROUPS : (h + 1) * GROUPS],
+                in_=by_capsule(g_times_s_of[(c, h)]),
+                axis=AXIS_X,
+                op=ALU.add,
+            )
 
         def factors(c):
             q = q_of[c]
@@ -195,15 +198,15 @@ def tile_capsulenetwork_pb_v_kernel(tc, p, Wr, s, grad_out, out):
             a_beta_of[c] = a_beta
 
         def scale_s_on_scalar(c):
-            h = PASSES - 1
-            s_t = s_of[(c, h)]
-            for t in range(PACK - SCALAR_ROWS, PACK):
-                for j in range(CAPSULES):
-                    group = h * GROUPS + t * CAPSULES + j
-                    values = s_t[:, t, j * CAP : (j + 1) * CAP]
-                    nc.scalar.activation(
-                        out=values, in_=values, func=ACT.Copy, scale=a_beta_of[c][:, 1, group : group + 1]
-                    )
+            for h in halves:
+                s_t = s_of[(c, h)]
+                for t in range(PACK - SCALAR_ROWS[h], PACK):
+                    for j in range(CAPSULES):
+                        group = h * GROUPS + t * CAPSULES + j
+                        values = s_t[:, t, j * CAP : (j + 1) * CAP]
+                        nc.scalar.activation(
+                            out=values, in_=values, func=ACT.Copy, scale=a_beta_of[c][:, 1, group : group + 1]
+                        )
 
         def scale_and_add(c):
             for h in halves:
@@ -217,16 +220,17 @@ def tile_capsulenetwork_pb_v_kernel(tc, p, Wr, s, grad_out, out):
                     in1=a_beta[:, 0, groups].unsqueeze(2).to_broadcast([P, GROUPS, CAP]),
                     op=ALU.mult,
                 )
-                rows = PACK - SCALAR_ROWS if (h == PASSES - 1 and c < CHUNKS - 1) else PACK
-                mine = s_t[:, 0:rows, :].rearrange("q t (j o) -> q (t j) o", o=CAP)
-                nc.vector.tensor_tensor(
-                    out=mine,
-                    in0=mine,
-                    in1=a_beta[:, 1, h * GROUPS : h * GROUPS + rows * CAPSULES]
-                    .unsqueeze(2)
-                    .to_broadcast([P, rows * CAPSULES, CAP]),
-                    op=ALU.mult,
-                )
+                rows = PACK - SCALAR_ROWS[h] if c < CHUNKS - 1 else PACK
+                if rows > 0:
+                    mine = s_t[:, 0:rows, :].rearrange("q t (j o) -> q (t j) o", o=CAP)
+                    nc.vector.tensor_tensor(
+                        out=mine,
+                        in0=mine,
+                        in1=a_beta[:, 1, h * GROUPS : h * GROUPS + rows * CAPSULES]
+                        .unsqueeze(2)
+                        .to_broadcast([P, rows * CAPSULES, CAP]),
+                        op=ALU.mult,
+                    )
                 ds_grouped = work.tile([P, CHUNK, PACK], BF16, align_bytes=64, bufs=2 * PASSES)
                 if (c, h) == (CHUNKS - 1, PASSES - 1):
                     quantise(c - 1)
@@ -316,30 +320,44 @@ def tile_capsulenetwork_pb_v_kernel(tc, p, Wr, s, grad_out, out):
         for h in halves:
             nc.sync.dma_start(out=p_raw[:, h], in_=p_rows[h])
         load(2)
-        square(0)
-        multiply_g_s(0)
-        sum_squares(0)
-        square(1)
+        for h in halves:
+            square(0, h)
+        for h in halves:
+            multiply_g_s(0, h, nc.gpsimd)
+        for h in halves:
+            sum_squares(0, h)
+        functions_of_q(0)
+        for h in halves:
+            square(1, h)
         for c in range(CHUNKS):
-            sum_products(c)
-            if c + 1 < CHUNKS:
-                multiply_g_s(c + 1)
+            more = c + 1 < CHUNKS
+            for h in reversed(halves):
+                sum_products(c, h)
+            if more:
+                multiply_g_s(c + 1, 0, nc.gpsimd)
             if c >= 2:
                 quantise(c - 2)
             factors(c)
+            if more:
+                scale_s_on_scalar(c)
+            if more:
+                multiply_g_s(c + 1, 1, nc.vector)
             if c == 1:
                 quantise_p()
             if c >= 2:
                 multiply(c - 2)
-            if c < CHUNKS - 1:
-                scale_s_on_scalar(c)
-            if c + 1 < CHUNKS:
-                sum_squares(c + 1)
+            scale_and_add(c)
+            if more:
+                for h in halves:
+                    sum_squares(c + 1, h)
             if c + 2 < CHUNKS:
-                square(c + 2)
+                square(c + 2, 0)
+            if more:
+                functions_of_q(c + 1)
             if c == 0:
                 regroup_p()
-            scale_and_add(c)
+            if c + 2 < CHUNKS:
+                square(c + 2, 1)
             if c + 3 < CHUNKS:
                 load(c + 3)
         quantise(CHUNKS - 1)

@@ -25,10 +25,12 @@ CHUNK = 512
 CHUNKS = COLS // CHUNK
 BLOCKS = CHUNK // P
 CAPSULES = CHUNK // CAP
-SCALAR_ROWS = (2, 4)
+SCALAR_ROWS = (1, 4)
+LAST_SCALAR_ROWS = (0, 2)
 GROUPS = PACK * (CHUNK // CAP)
 GPSIMD_COLS = 384
 SQ_EPS = 1e-8
+ROOT_EPS = 1e-4
 COUPLING = 1.0 / 256.0
 
 FLOPS = 2 * BATCH * NI * COLS
@@ -66,7 +68,7 @@ def tile_capsulenetwork_pb_v_kernel(tc, p, Wr, s, grad_out, out):
         q_of = {}
         r_of = {}
         w_of = {}
-        q_r2_of = {}
+        eps_r2_of = {}
         d_of = {}
         factors_of = {}
         a_beta_of = {}
@@ -86,8 +88,11 @@ def tile_capsulenetwork_pb_v_kernel(tc, p, Wr, s, grad_out, out):
         p_scales = const.tile([P, PASSES, NI], U8, align_bytes=64)
 
         def pieces(c, h):
-            step = PACK // 2 if (c, h) == (0, 0) else PACK
+            step = PACK // 2 if c == 0 else PACK
             return [slice(t, t + step) for t in range(0, PACK, step)]
+
+        def scalar_rows(c, h):
+            return (SCALAR_ROWS if c < CHUNKS - 1 else LAST_SCALAR_ROWS)[h]
 
         def load(c):
             cols = slice(c * CHUNK, (c + 1) * CHUNK)
@@ -149,15 +154,11 @@ def tile_capsulenetwork_pb_v_kernel(tc, p, Wr, s, grad_out, out):
             nc.scalar.activation(out=q1_squared[:], in_=q[:], func=ACT.Square, bias=one[:, 0:1])
             w = small.tile([P, PASSES * GROUPS], F32)
             nc.scalar.activation(out=w[:], in_=q1_squared[:], func=ACT.Abs_reciprocal_sqrt)
-            r_squared = small.tile([P, PASSES * GROUPS], F32)
-            nc.scalar.activation(out=r_squared[:], in_=r[:], func=ACT.Square)
-            q_r2 = small.tile([P, PASSES * GROUPS], F32)
-            nc.scalar.activation(
-                out=q_r2[:], in_=r_squared[:], func=ACT.Identity, scale=-SQ_EPS, bias=one[:, 0:1]
-            )
+            eps_r2 = small.tile([P, PASSES * GROUPS], F32)
+            nc.scalar.activation(out=eps_r2[:], in_=r[:], func=ACT.Square, scale=ROOT_EPS)
             r_of[c] = r
             w_of[c] = w
-            q_r2_of[c] = q_r2
+            eps_r2_of[c] = eps_r2
 
         def sum_products(c, h):
             if c not in d_of:
@@ -177,15 +178,17 @@ def tile_capsulenetwork_pb_v_kernel(tc, p, Wr, s, grad_out, out):
             width = [P, PASSES * GROUPS]
             z = small.tile(width, F32)
             nc.vector.tensor_tensor(out=z[:], in0=w[:], in1=r_of[c][:], op=ALU.mult)
-            bracket = small.tile(width, F32)
+            bracket_1 = small.tile(width, F32)
             nc.vector.scalar_tensor_tensor(
-                out=bracket[:], in0=w[:], scalar=2.0, in1=q_r2_of[c][:], op0=ALU.mult, op1=ALU.subtract
+                out=bracket_1[:], in0=w[:], scalar=2.0, in1=eps_r2_of[c][:], op0=ALU.mult, op1=ALU.add
             )
             z_d = small.tile(width, F32)
             nc.vector.tensor_tensor(out=z_d[:], in0=z[:], in1=d_of[c][:], op=ALU.mult)
             a_beta = small.tile([P, 2, PASSES * GROUPS], F32)
             nc.vector.tensor_tensor(out=a_beta[:, 0, :], in0=q[:], in1=z[:], op=ALU.mult)
-            nc.vector.tensor_tensor(out=a_beta[:, 1, :], in0=z_d[:], in1=bracket[:], op=ALU.mult)
+            nc.vector.scalar_tensor_tensor(
+                out=a_beta[:, 1, :], in0=bracket_1[:], scalar=-1.0, in1=z_d[:], op0=ALU.add, op1=ALU.mult
+            )
             a_beta_psum = factor_banks.tile([P, 2, PASSES * GROUPS], F32)
             nc.tensor.matmul(
                 out=a_beta_psum[:].rearrange("q k x -> q (k x)"),
@@ -200,7 +203,7 @@ def tile_capsulenetwork_pb_v_kernel(tc, p, Wr, s, grad_out, out):
         def scale_s_on_scalar(c):
             for h in halves:
                 s_t = s_of[(c, h)]
-                for t in range(PACK - SCALAR_ROWS[h], PACK):
+                for t in range(PACK - scalar_rows(c, h), PACK):
                     for j in range(CAPSULES):
                         group = h * GROUPS + t * CAPSULES + j
                         values = s_t[:, t, j * CAP : (j + 1) * CAP]
@@ -220,7 +223,7 @@ def tile_capsulenetwork_pb_v_kernel(tc, p, Wr, s, grad_out, out):
                     in1=a_beta[:, 0, groups].unsqueeze(2).to_broadcast([P, GROUPS, CAP]),
                     op=ALU.mult,
                 )
-                rows = PACK - SCALAR_ROWS[h] if c < CHUNKS - 1 else PACK
+                rows = PACK - scalar_rows(c, h)
                 if rows > 0:
                     mine = s_t[:, 0:rows, :].rearrange("q t (j o) -> q (t j) o", o=CAP)
                     nc.vector.tensor_tensor(
@@ -233,7 +236,6 @@ def tile_capsulenetwork_pb_v_kernel(tc, p, Wr, s, grad_out, out):
                     )
                 ds_grouped = work.tile([P, CHUNK, PACK], BF16, align_bytes=64, bufs=2 * PASSES)
                 if (c, h) == (CHUNKS - 1, PASSES - 1):
-                    quantise(c - 1)
                     multiply(c - 1)
                     nc.vector.tensor_tensor(
                         out=ds_grouped[:].rearrange("q (m w) t -> q m w t", m=BLOCKS),
@@ -322,8 +324,8 @@ def tile_capsulenetwork_pb_v_kernel(tc, p, Wr, s, grad_out, out):
         load(2)
         for h in halves:
             square(0, h)
-        for h in halves:
-            multiply_g_s(0, h, nc.gpsimd)
+        multiply_g_s(0, 0, nc.vector)
+        multiply_g_s(0, 1, nc.gpsimd)
         for h in halves:
             sum_squares(0, h)
         functions_of_q(0)
@@ -340,12 +342,15 @@ def tile_capsulenetwork_pb_v_kernel(tc, p, Wr, s, grad_out, out):
             factors(c)
             if more:
                 scale_s_on_scalar(c)
-            if more:
                 multiply_g_s(c + 1, 1, nc.vector)
+            else:
+                quantise(c - 1)
             if c == 1:
                 quantise_p()
             if c >= 2:
                 multiply(c - 2)
+            if not more:
+                scale_s_on_scalar(c)
             scale_and_add(c)
             if more:
                 for h in halves:

@@ -26,6 +26,7 @@ CHUNKS = COLS // CHUNK
 BLOCKS = CHUNK // P
 CAPSULES = CHUNK // CAP
 SCALAR_ROWS = (1, 4)
+VECTOR_ROWS = 3
 LAST_SCALAR_ROWS = (0, 2)
 GROUPS = PACK * (CHUNK // CAP)
 GPSIMD_COLS = 384
@@ -56,7 +57,7 @@ def tile_capsulenetwork_pb_v_kernel(tc, p, Wr, s, grad_out, out):
         stream = stack.enter_context(tc.tile_pool(name="stream", bufs=6))
         work = stack.enter_context(tc.tile_pool(name="work", bufs=2))
         small = stack.enter_context(tc.tile_pool(name="small", bufs=2))
-        factor_banks = stack.enter_context(tc.psum_pool(name="factor_banks", bufs=2))
+        factor_banks = stack.enter_context(tc.psum_pool(name="factor_banks", bufs=1))
         product_banks = stack.enter_context(tc.psum_pool(name="product_banks", bufs=4))
         sum_banks = stack.enter_context(tc.psum_pool(name="sum_banks", bufs=2))
         stack.enter_context(tc.manual_schedule())
@@ -122,16 +123,17 @@ def tile_capsulenetwork_pb_v_kernel(tc, p, Wr, s, grad_out, out):
                 nc.scalar.activation(out=squares[:, rows, :], in_=s_of[(c, h)][:, rows, :], func=ACT.Square)
             squares_of[(c, h)] = squares
 
-        def multiply_g_s(c, h, engine):
-            g_times_s = work.tile([P, PACK, CHUNK], F32)
-            for rows in pieces(c, h):
+        def multiply_g_s(engine, c, h, spans):
+            if (c, h) not in g_times_s_of:
+                g_times_s = work.tile([P, PACK, CHUNK], F32, name="product_%d" % h, bufs=1)
+                g_times_s_of[(c, h)] = g_times_s
+            for rows in spans:
                 engine.tensor_tensor(
-                    out=g_times_s[:, rows, :],
+                    out=g_times_s_of[(c, h)][:, rows, :],
                     in0=g_of[(c, h)][:, rows, :],
                     in1=s_of[(c, h)][:, rows, :],
                     op=ALU.mult,
                 )
-            g_times_s_of[(c, h)] = g_times_s
 
         def sum_squares(c, h):
             if h == 0:
@@ -182,22 +184,34 @@ def tile_capsulenetwork_pb_v_kernel(tc, p, Wr, s, grad_out, out):
             nc.vector.scalar_tensor_tensor(
                 out=bracket_1[:], in0=w[:], scalar=2.0, in1=eps_r2_of[c][:], op0=ALU.mult, op1=ALU.add
             )
-            z_d = small.tile(width, F32)
+            z_d = work.tile(width, F32, name="product_0", bufs=1)
             nc.vector.tensor_tensor(out=z_d[:], in0=z[:], in1=d_of[c][:], op=ALU.mult)
-            a_beta = small.tile([P, 2, PASSES * GROUPS], F32)
-            nc.vector.tensor_tensor(out=a_beta[:, 0, :], in0=q[:], in1=z[:], op=ALU.mult)
+            a_beta = small.tile([P, PASSES, 2, GROUPS], F32)
+            by_half = "q (h x) -> q h x"
+            nc.vector.tensor_tensor(
+                out=a_beta[:, :, 0, :],
+                in0=q[:].rearrange(by_half, h=PASSES),
+                in1=z[:].rearrange(by_half, h=PASSES),
+                op=ALU.mult,
+            )
             nc.vector.scalar_tensor_tensor(
-                out=a_beta[:, 1, :], in0=bracket_1[:], scalar=-1.0, in1=z_d[:], op0=ALU.add, op1=ALU.mult
+                out=a_beta[:, :, 1, :],
+                in0=bracket_1[:].rearrange(by_half, h=PASSES),
+                scalar=-1.0,
+                in1=z_d[:].rearrange(by_half, h=PASSES),
+                op0=ALU.add,
+                op1=ALU.mult,
             )
-            a_beta_psum = factor_banks.tile([P, 2, PASSES * GROUPS], F32)
-            nc.tensor.matmul(
-                out=a_beta_psum[:].rearrange("q k x -> q (k x)"),
-                lhsT=identity[:],
-                rhs=a_beta[:].rearrange("q k x -> q (k x)"),
-                start=True,
-                stop=True,
-            )
-            factors_of[c] = a_beta_psum
+            for h in halves:
+                a_beta_psum = factor_banks.tile([P, 2, GROUPS], F32, name="factors_%d" % h)
+                nc.tensor.matmul(
+                    out=a_beta_psum[:].rearrange("q k x -> q (k x)"),
+                    lhsT=identity[:],
+                    rhs=a_beta[:, h].rearrange("q k x -> q (k x)"),
+                    start=True,
+                    stop=True,
+                )
+                factors_of[(c, h)] = a_beta_psum
             a_beta_of[c] = a_beta
 
         def scale_s_on_scalar(c):
@@ -205,22 +219,21 @@ def tile_capsulenetwork_pb_v_kernel(tc, p, Wr, s, grad_out, out):
                 s_t = s_of[(c, h)]
                 for t in range(PACK - scalar_rows(c, h), PACK):
                     for j in range(CAPSULES):
-                        group = h * GROUPS + t * CAPSULES + j
+                        group = t * CAPSULES + j
                         values = s_t[:, t, j * CAP : (j + 1) * CAP]
                         nc.scalar.activation(
-                            out=values, in_=values, func=ACT.Copy, scale=a_beta_of[c][:, 1, group : group + 1]
+                            out=values, in_=values, func=ACT.Copy, scale=a_beta_of[c][:, h, 1, group : group + 1]
                         )
 
         def scale_and_add(c):
             for h in halves:
-                groups = slice(h * GROUPS, (h + 1) * GROUPS)
                 s_t = s_of[(c, h)]
-                a_beta = a_beta_of[c] if (c == CHUNKS - 1 and h == 0) else factors_of[c]
+                a_beta = a_beta_of[c][:, h] if (c == CHUNKS - 1 and h == 0) else factors_of[(c, h)]
                 a_g = work.tile([P, PACK, CHUNK], F32)
                 nc.vector.tensor_tensor(
                     out=by_capsule(a_g),
                     in0=by_capsule(g_of[(c, h)]),
-                    in1=a_beta[:, 0, groups].unsqueeze(2).to_broadcast([P, GROUPS, CAP]),
+                    in1=a_beta[:, 0, :].unsqueeze(2).to_broadcast([P, GROUPS, CAP]),
                     op=ALU.mult,
                 )
                 rows = PACK - scalar_rows(c, h)
@@ -229,24 +242,27 @@ def tile_capsulenetwork_pb_v_kernel(tc, p, Wr, s, grad_out, out):
                     nc.vector.tensor_tensor(
                         out=mine,
                         in0=mine,
-                        in1=a_beta[:, 1, h * GROUPS : h * GROUPS + rows * CAPSULES]
+                        in1=a_beta[:, 1, 0 : rows * CAPSULES]
                         .unsqueeze(2)
                         .to_broadcast([P, rows * CAPSULES, CAP]),
                         op=ALU.mult,
                     )
-                ds_grouped = work.tile([P, CHUNK, PACK], BF16, align_bytes=64, bufs=2 * PASSES)
+                if h == 0:
+                    ds_both = work.tile([P, PASSES, CHUNK, PACK], BF16, align_bytes=64)
+                    grouped_of[c] = ds_both
+                ds_grouped = grouped_of[c][:, h]
                 if (c, h) == (CHUNKS - 1, PASSES - 1):
                     multiply(c - 1)
                     nc.vector.tensor_tensor(
-                        out=ds_grouped[:].rearrange("q (m w) t -> q m w t", m=BLOCKS),
+                        out=ds_grouped.rearrange("q (m w) t -> q m w t", m=BLOCKS),
                         in0=a_g[:].rearrange("q t (w m) -> q m w t", m=BLOCKS),
                         in1=s_t[:].rearrange("q t (w m) -> q m w t", m=BLOCKS),
                         op=ALU.add,
                     )
                 elif h == 0:
-                    grouped = ds_grouped[:].rearrange("q (m w) t -> q m w t", m=BLOCKS)
+                    grouped = ds_grouped.rearrange("q (m w) t -> q m w t", m=BLOCKS)
                     nc.gpsimd.tensor_tensor(
-                        out=ds_grouped[:].rearrange("q (m w) t -> q w t m", m=BLOCKS)[:, 0 : GPSIMD_COLS // BLOCKS],
+                        out=ds_grouped.rearrange("q (m w) t -> q w t m", m=BLOCKS)[:, 0 : GPSIMD_COLS // BLOCKS],
                         in0=a_g[:, :, 0:GPSIMD_COLS].rearrange("q t (w m) -> q w t m", m=BLOCKS),
                         in1=s_t[:, :, 0:GPSIMD_COLS].rearrange("q t (w m) -> q w t m", m=BLOCKS),
                         op=ALU.add,
@@ -264,21 +280,21 @@ def tile_capsulenetwork_pb_v_kernel(tc, p, Wr, s, grad_out, out):
                     )
                 else:
                     nc.gpsimd.tensor_tensor(
-                        out=ds_grouped[:].rearrange("q (m w) t -> q w t m", m=BLOCKS),
+                        out=ds_grouped.rearrange("q (m w) t -> q w t m", m=BLOCKS),
                         in0=a_g[:].rearrange("q t (w m) -> q w t m", m=BLOCKS),
                         in1=s_t[:].rearrange("q t (w m) -> q w t m", m=BLOCKS),
                         op=ALU.add,
                     )
-                grouped_of[(c, h)] = ds_grouped
 
         def quantise(c):
             ds_codes = work.tile([P, PASSES, CHUNK], U32, align_bytes=64)
             ds_scales = work.tile([P, PASSES, CHUNK], U8, align_bytes=64)
-            for h in halves:
+            for hs in [halves] if c < CHUNKS - 1 else [halves[0:1], halves[1:2]]:
+                span = slice(hs.start, hs.stop)
                 nc.vector.quantize_mx(
-                    out=ds_codes[:, h, :].bitcast(E5M2X4),
-                    scales=ds_scales[:, h, :],
-                    in_=grouped_of[(c, h)][:].rearrange("q w t -> q (w t)"),
+                    out=ds_codes[:, span, :].rearrange("q h w -> q (h w)").bitcast(E5M2X4),
+                    scales=ds_scales[:, span, :].rearrange("q h w -> q (h w)"),
+                    in_=grouped_of[c][:, span].rearrange("q h w t -> q (h w t)"),
                 )
             codes_of[c] = ds_codes
             scales_of[c] = ds_scales
@@ -324,8 +340,8 @@ def tile_capsulenetwork_pb_v_kernel(tc, p, Wr, s, grad_out, out):
         load(2)
         for h in halves:
             square(0, h)
-        multiply_g_s(0, 0, nc.vector)
-        multiply_g_s(0, 1, nc.gpsimd)
+        multiply_g_s(nc.vector, 0, 0, pieces(0, 0))
+        multiply_g_s(nc.gpsimd, 0, 1, pieces(0, 1))
         for h in halves:
             sum_squares(0, h)
         functions_of_q(0)
@@ -336,14 +352,16 @@ def tile_capsulenetwork_pb_v_kernel(tc, p, Wr, s, grad_out, out):
             for h in reversed(halves):
                 sum_products(c, h)
             if more:
-                multiply_g_s(c + 1, 0, nc.gpsimd)
-            if c >= 2:
-                quantise(c - 2)
+                multiply_g_s(nc.vector, c + 1, 1, [slice(0, VECTOR_ROWS)])
             factors(c)
             if more:
                 scale_s_on_scalar(c)
-                multiply_g_s(c + 1, 1, nc.vector)
-            else:
+                multiply_g_s(nc.gpsimd, c + 1, 0, [slice(0, PACK)])
+                if VECTOR_ROWS < PACK:
+                    multiply_g_s(nc.gpsimd, c + 1, 1, [slice(VECTOR_ROWS, PACK)])
+            if c >= 2:
+                quantise(c - 2)
+            if not more:
                 quantise(c - 1)
             if c == 1:
                 quantise_p()

@@ -26,7 +26,7 @@ CHUNKS = COLS // CHUNK
 BLOCKS = CHUNK // P
 CAPSULES = CHUNK // CAP
 SCALAR_ROWS = (1, 4)
-VECTOR_ROWS = 3
+VECTOR_ROWS = 2
 LAST_SCALAR_ROWS = (0, 2)
 GROUPS = PACK * (CHUNK // CAP)
 GPSIMD_COLS = 384
@@ -38,8 +38,12 @@ FLOPS = 2 * BATCH * NI * COLS
 BYTES = BATCH * NI * 2 + BATCH * COLS * (4 + 2) + NI * COLS * 4
 
 
-def by_capsule(tile):
-    return tile[:].rearrange("q t (j o) -> q (t j) o", o=CAP)
+def by_capsule(values):
+    return values.rearrange("q t (j o) -> q (t j) o", o=CAP)
+
+
+def on_capsules(factors, count):
+    return factors.unsqueeze(2).to_broadcast([P, count, CAP])
 
 
 def tile_capsulenetwork_pb_v_kernel(tc, p, Wr, s, grad_out, out):
@@ -54,7 +58,7 @@ def tile_capsulenetwork_pb_v_kernel(tc, p, Wr, s, grad_out, out):
 
     with ExitStack() as stack:
         const = stack.enter_context(tc.tile_pool(name="const", bufs=1))
-        stream = stack.enter_context(tc.tile_pool(name="stream", bufs=6))
+        stream = stack.enter_context(tc.tile_pool(name="stream", bufs=3))
         work = stack.enter_context(tc.tile_pool(name="work", bufs=2))
         small = stack.enter_context(tc.tile_pool(name="small", bufs=2))
         factor_banks = stack.enter_context(tc.psum_pool(name="factor_banks", bufs=1))
@@ -71,8 +75,10 @@ def tile_capsulenetwork_pb_v_kernel(tc, p, Wr, s, grad_out, out):
         w_of = {}
         eps_r2_of = {}
         d_of = {}
-        factors_of = {}
+        a_of = {}
+        beta_of = {}
         a_beta_of = {}
+        a_g_of = {}
         grouped_of = {}
         codes_of = {}
         scales_of = {}
@@ -88,7 +94,7 @@ def tile_capsulenetwork_pb_v_kernel(tc, p, Wr, s, grad_out, out):
         p_codes = const.tile([P, PASSES, NI], U32, align_bytes=64)
         p_scales = const.tile([P, PASSES, NI], U8, align_bytes=64)
 
-        def pieces(c, h):
+        def pieces(c):
             step = PACK // 2 if c == 0 else PACK
             return [slice(t, t + step) for t in range(0, PACK, step)]
 
@@ -97,14 +103,14 @@ def tile_capsulenetwork_pb_v_kernel(tc, p, Wr, s, grad_out, out):
 
         def load(c):
             cols = slice(c * CHUNK, (c + 1) * CHUNK)
+            s_t = stream.tile([P, PASSES, PACK, CHUNK], F32)
+            g_t = stream.tile([P, PASSES, PACK, CHUNK], BF16)
             for h in halves:
-                s_t = stream.tile([P, PACK, CHUNK], F32)
-                g_t = stream.tile([P, PACK, CHUNK], BF16)
-                for rows in pieces(c, h):
-                    nc.sync.dma_start(out=s_t[:, rows, :], in_=s_rows[h, :, rows, cols])
-                    nc.sync.dma_start(out=g_t[:, rows, :], in_=g_rows[h, :, rows, cols])
-                s_of[(c, h)] = s_t
-                g_of[(c, h)] = g_t
+                for rows in pieces(c):
+                    nc.sync.dma_start(out=s_t[:, h, rows, :], in_=s_rows[h, :, rows, cols])
+                    nc.sync.dma_start(out=g_t[:, h, rows, :], in_=g_rows[h, :, rows, cols])
+            s_of[c] = s_t
+            g_of[c] = g_t
 
         def regroup_p():
             for h in halves:
@@ -118,10 +124,13 @@ def tile_capsulenetwork_pb_v_kernel(tc, p, Wr, s, grad_out, out):
             )
 
         def square(c, h):
-            squares = work.tile([P, PACK, CHUNK], F32)
-            for rows in pieces(c, h):
-                nc.scalar.activation(out=squares[:, rows, :], in_=s_of[(c, h)][:, rows, :], func=ACT.Square)
-            squares_of[(c, h)] = squares
+            if h == 0:
+                squares = work.tile([P, PASSES, PACK, CHUNK], F32, bufs=2)
+                squares_of[c] = squares
+            for rows in pieces(c):
+                nc.scalar.activation(
+                    out=squares_of[c][:, h, rows, :], in_=s_of[c][:, h, rows, :], func=ACT.Square
+                )
 
         def multiply_g_s(engine, c, h, spans):
             if (c, h) not in g_times_s_of:
@@ -130,23 +139,31 @@ def tile_capsulenetwork_pb_v_kernel(tc, p, Wr, s, grad_out, out):
             for rows in spans:
                 engine.tensor_tensor(
                     out=g_times_s_of[(c, h)][:, rows, :],
-                    in0=g_of[(c, h)][:, rows, :],
-                    in1=s_of[(c, h)][:, rows, :],
+                    in0=g_of[c][:, h, rows, :],
+                    in1=s_of[c][:, h, rows, :],
                     op=ALU.mult,
                 )
 
-        def sum_squares(c, h):
-            if h == 0:
-                q = small.tile([P, PASSES * GROUPS], F32)
-                q_of[c] = q
-            q = q_of[c]
-            for rows in pieces(c, h):
+        def sum_squares(c):
+            q = small.tile([P, PASSES * GROUPS], F32)
+            q_of[c] = q
+            if c > 0:
                 nc.vector.tensor_reduce(
-                    out=q[:, h * GROUPS + rows.start * CAPSULES : h * GROUPS + rows.stop * CAPSULES],
-                    in_=squares_of[(c, h)][:, rows, :].rearrange("q t (j o) -> q (t j) o", o=CAP),
+                    out=q[:],
+                    in_=squares_of[c][:].rearrange("q h t (j o) -> q (h t j) o", o=CAP),
                     axis=AXIS_X,
                     op=ALU.add,
                 )
+                return
+            for h in halves:
+                for rows in pieces(c):
+                    first = h * GROUPS + rows.start * CAPSULES
+                    nc.vector.tensor_reduce(
+                        out=q[:, first : first + (rows.stop - rows.start) * CAPSULES],
+                        in_=by_capsule(squares_of[c][:, h, rows, :]),
+                        axis=AXIS_X,
+                        op=ALU.add,
+                    )
 
         def functions_of_q(c):
             q = q_of[c]
@@ -169,7 +186,7 @@ def tile_capsulenetwork_pb_v_kernel(tc, p, Wr, s, grad_out, out):
             d = d_of[c]
             nc.vector.tensor_reduce(
                 out=d[:, h * GROUPS : (h + 1) * GROUPS],
-                in_=by_capsule(g_times_s_of[(c, h)]),
+                in_=by_capsule(g_times_s_of[(c, h)][:]),
                 axis=AXIS_X,
                 op=ALU.add,
             )
@@ -202,89 +219,96 @@ def tile_capsulenetwork_pb_v_kernel(tc, p, Wr, s, grad_out, out):
                 op0=ALU.add,
                 op1=ALU.mult,
             )
-            for h in halves:
-                a_beta_psum = factor_banks.tile([P, 2, GROUPS], F32, name="factors_%d" % h)
+            a_psum = factor_banks.tile([P, PASSES, GROUPS], F32)
+            nc.tensor.matmul(out=a_psum[:], lhsT=identity[:], rhs=a_beta[:, :, 0, :], start=True, stop=True)
+            a_of[c] = a_psum
+            beta_psum = factor_banks.tile([P, PASSES, GROUPS], F32)
+            if c < CHUNKS - 1:
+                mine = (PACK - SCALAR_ROWS[0]) * CAPSULES
                 nc.tensor.matmul(
-                    out=a_beta_psum[:].rearrange("q k x -> q (k x)"),
+                    out=beta_psum[:, 0, 0:mine],
                     lhsT=identity[:],
-                    rhs=a_beta[:, h].rearrange("q k x -> q (k x)"),
+                    rhs=a_beta[:, 0, 1, 0:mine],
                     start=True,
                     stop=True,
                 )
-                factors_of[(c, h)] = a_beta_psum
+            else:
+                nc.tensor.matmul(
+                    out=beta_psum[:], lhsT=identity[:], rhs=a_beta[:, :, 1, :], start=True, stop=True
+                )
+            beta_of[c] = beta_psum
             a_beta_of[c] = a_beta
 
         def scale_s_on_scalar(c):
             for h in halves:
-                s_t = s_of[(c, h)]
                 for t in range(PACK - scalar_rows(c, h), PACK):
                     for j in range(CAPSULES):
                         group = t * CAPSULES + j
-                        values = s_t[:, t, j * CAP : (j + 1) * CAP]
+                        values = s_of[c][:, h, t, j * CAP : (j + 1) * CAP]
                         nc.scalar.activation(
                             out=values, in_=values, func=ACT.Copy, scale=a_beta_of[c][:, h, 1, group : group + 1]
                         )
 
-        def scale_and_add(c):
-            for h in halves:
-                s_t = s_of[(c, h)]
-                a_beta = a_beta_of[c][:, h] if (c == CHUNKS - 1 and h == 0) else factors_of[(c, h)]
-                a_g = work.tile([P, PACK, CHUNK], F32)
+        def scale(c):
+            a_g = work.tile([P, PASSES, PACK, CHUNK], F32, bufs=1)
+            a_g_of[c] = a_g
+            if c < CHUNKS - 1:
                 nc.vector.tensor_tensor(
-                    out=by_capsule(a_g),
-                    in0=by_capsule(g_of[(c, h)]),
-                    in1=a_beta[:, 0, :].unsqueeze(2).to_broadcast([P, GROUPS, CAP]),
+                    out=a_g[:].rearrange("q h t (j o) -> q (h t j) o", o=CAP),
+                    in0=g_of[c][:].rearrange("q h t (j o) -> q (h t j) o", o=CAP),
+                    in1=on_capsules(a_of[c][:].rearrange("q h x -> q (h x)"), PASSES * GROUPS),
                     op=ALU.mult,
                 )
-                rows = PACK - scalar_rows(c, h)
-                if rows > 0:
-                    mine = s_t[:, 0:rows, :].rearrange("q t (j o) -> q (t j) o", o=CAP)
+            for h in halves:
+                if c == CHUNKS - 1:
+                    a, beta = (
+                        (a_beta_of[c][:, h, 0, :], a_beta_of[c][:, h, 1, :])
+                        if h == 0
+                        else (a_of[c][:, h, :], beta_of[c][:, h, :])
+                    )
                     nc.vector.tensor_tensor(
-                        out=mine,
-                        in0=mine,
-                        in1=a_beta[:, 1, 0 : rows * CAPSULES]
-                        .unsqueeze(2)
-                        .to_broadcast([P, rows * CAPSULES, CAP]),
-                        op=ALU.mult,
-                    )
-                if h == 0:
-                    ds_both = work.tile([P, PASSES, CHUNK, PACK], BF16, align_bytes=64)
-                    grouped_of[c] = ds_both
-                ds_grouped = grouped_of[c][:, h]
-                if (c, h) == (CHUNKS - 1, PASSES - 1):
-                    multiply(c - 1)
-                    nc.vector.tensor_tensor(
-                        out=ds_grouped.rearrange("q (m w) t -> q m w t", m=BLOCKS),
-                        in0=a_g[:].rearrange("q t (w m) -> q m w t", m=BLOCKS),
-                        in1=s_t[:].rearrange("q t (w m) -> q m w t", m=BLOCKS),
-                        op=ALU.add,
-                    )
-                elif h == 0:
-                    grouped = ds_grouped.rearrange("q (m w) t -> q m w t", m=BLOCKS)
-                    nc.gpsimd.tensor_tensor(
-                        out=ds_grouped.rearrange("q (m w) t -> q w t m", m=BLOCKS)[:, 0 : GPSIMD_COLS // BLOCKS],
-                        in0=a_g[:, :, 0:GPSIMD_COLS].rearrange("q t (w m) -> q w t m", m=BLOCKS),
-                        in1=s_t[:, :, 0:GPSIMD_COLS].rearrange("q t (w m) -> q w t m", m=BLOCKS),
-                        op=ALU.add,
-                    )
-                    rest = sum_banks.tile([P, PACK, CHUNK - GPSIMD_COLS], F32)
-                    nc.tensor.matmul(
-                        out=rest[:], lhsT=identity[:], rhs=a_g[:, :, GPSIMD_COLS:CHUNK], start=True, stop=False
-                    )
-                    nc.tensor.matmul(
-                        out=rest[:], lhsT=identity[:], rhs=s_t[:, :, GPSIMD_COLS:CHUNK], start=False, stop=True
-                    )
-                    nc.scalar.copy(
-                        out=grouped[:, :, GPSIMD_COLS // BLOCKS : P, :],
-                        in_=rest[:].rearrange("q t (w m) -> q m w t", m=BLOCKS),
+                        out=by_capsule(a_g[:, h]), in0=by_capsule(g_of[c][:, h]), in1=on_capsules(a, GROUPS), op=ALU.mult
                     )
                 else:
-                    nc.gpsimd.tensor_tensor(
-                        out=ds_grouped.rearrange("q (m w) t -> q w t m", m=BLOCKS),
-                        in0=a_g[:].rearrange("q t (w m) -> q w t m", m=BLOCKS),
-                        in1=s_t[:].rearrange("q t (w m) -> q w t m", m=BLOCKS),
-                        op=ALU.add,
+                    beta = beta_of[c][:, h, :]
+                rows = PACK - scalar_rows(c, h)
+                if rows > 0:
+                    mine = by_capsule(s_of[c][:, h, 0:rows, :])
+                    nc.vector.tensor_tensor(
+                        out=mine, in0=mine, in1=on_capsules(beta[:, 0 : rows * CAPSULES], rows * CAPSULES), op=ALU.mult
                     )
+
+        def add(c, h):
+            if h == 0:
+                ds_grouped = work.tile([P, PASSES, CHUNK, PACK], BF16, align_bytes=64)
+                grouped_of[c] = ds_grouped
+            a_g = a_g_of[c][:, h]
+            beta_s = s_of[c][:, h]
+            walk = "q (m w) t -> q w t m"
+            natural = "q t (w m) -> q w t m"
+            if (c, h) == (CHUNKS - 1, PASSES - 1):
+                nc.vector.tensor_tensor(
+                    out=grouped_of[c][:, h].rearrange("q (m w) t -> q m w t", m=BLOCKS),
+                    in0=a_g.rearrange("q t (w m) -> q m w t", m=BLOCKS),
+                    in1=beta_s.rearrange("q t (w m) -> q m w t", m=BLOCKS),
+                    op=ALU.add,
+                )
+                return
+            cols = GPSIMD_COLS if h == 0 else CHUNK
+            nc.gpsimd.tensor_tensor(
+                out=grouped_of[c][:, h].rearrange(walk, m=BLOCKS)[:, 0 : cols // BLOCKS],
+                in0=a_g[:, :, 0:cols].rearrange(natural, m=BLOCKS),
+                in1=beta_s[:, :, 0:cols].rearrange(natural, m=BLOCKS),
+                op=ALU.add,
+            )
+            if cols < CHUNK:
+                rest = sum_banks.tile([P, PACK, CHUNK - GPSIMD_COLS], F32)
+                nc.tensor.matmul(out=rest[:], lhsT=identity[:], rhs=a_g[:, :, cols:CHUNK], start=True, stop=False)
+                nc.tensor.matmul(out=rest[:], lhsT=identity[:], rhs=beta_s[:, :, cols:CHUNK], start=False, stop=True)
+                nc.scalar.copy(
+                    out=grouped_of[c][:, h].rearrange("q (m w) t -> q m w t", m=BLOCKS)[:, :, cols // BLOCKS : P, :],
+                    in_=rest[:].rearrange("q t (w m) -> q m w t", m=BLOCKS),
+                )
 
         def quantise(c):
             ds_codes = work.tile([P, PASSES, CHUNK], U32, align_bytes=64)
@@ -340,10 +364,9 @@ def tile_capsulenetwork_pb_v_kernel(tc, p, Wr, s, grad_out, out):
         load(2)
         for h in halves:
             square(0, h)
-        multiply_g_s(nc.vector, 0, 0, pieces(0, 0))
-        multiply_g_s(nc.gpsimd, 0, 1, pieces(0, 1))
-        for h in halves:
-            sum_squares(0, h)
+        multiply_g_s(nc.vector, 0, 0, pieces(0))
+        multiply_g_s(nc.gpsimd, 0, 1, pieces(0))
+        sum_squares(0)
         functions_of_q(0)
         for h in halves:
             square(1, h)
@@ -369,10 +392,13 @@ def tile_capsulenetwork_pb_v_kernel(tc, p, Wr, s, grad_out, out):
                 multiply(c - 2)
             if not more:
                 scale_s_on_scalar(c)
-            scale_and_add(c)
+            scale(c)
+            for h in halves:
+                if (c, h) == (CHUNKS - 1, PASSES - 1):
+                    multiply(c - 1)
+                add(c, h)
             if more:
-                for h in halves:
-                    sum_squares(c + 1, h)
+                sum_squares(c + 1)
             if c + 2 < CHUNKS:
                 square(c + 2, 0)
             if more:

@@ -25,10 +25,12 @@ CHUNK = 512
 CHUNKS = COLS // CHUNK
 BLOCKS = CHUNK // P
 CAPSULES = CHUNK // CAP
-SCALAR_ROWS = (1, 4)
-VECTOR_ROWS = 2
-LAST_SCALAR_ROWS = (0, 2)
-GROUPS = PACK * (CHUNK // CAP)
+ROWS = PASSES * PACK
+GROUPS = ROWS * CAPSULES
+HALF = GROUPS // PASSES
+VECTOR_SCALES = 96
+LAST_VECTOR_SCALES = 192
+GPSIMD_PRODUCTS = 192
 GPSIMD_COLS = 384
 SQ_EPS = 1e-8
 ROOT_EPS = 1e-4
@@ -39,7 +41,7 @@ BYTES = BATCH * NI * 2 + BATCH * COLS * (4 + 2) + NI * COLS * 4
 
 
 def by_capsule(values):
-    return values.rearrange("q t (j o) -> q (t j) o", o=CAP)
+    return values.rearrange("q r (j o) -> q (r j) o", o=CAP)
 
 
 def on_capsules(factors, count):
@@ -75,8 +77,7 @@ def tile_capsulenetwork_pb_v_kernel(tc, p, Wr, s, grad_out, out):
         w_of = {}
         eps_r2_of = {}
         d_of = {}
-        a_of = {}
-        beta_of = {}
+        factor_of = {}
         a_beta_of = {}
         a_g_of = {}
         grouped_of = {}
@@ -96,19 +97,17 @@ def tile_capsulenetwork_pb_v_kernel(tc, p, Wr, s, grad_out, out):
 
         def pieces(c):
             step = PACK // 2 if c == 0 else PACK
-            return [slice(t, t + step) for t in range(0, PACK, step)]
-
-        def scalar_rows(c, h):
-            return (SCALAR_ROWS if c < CHUNKS - 1 else LAST_SCALAR_ROWS)[h]
+            return [slice(r, r + step) for r in range(0, ROWS, step)]
 
         def load(c):
             cols = slice(c * CHUNK, (c + 1) * CHUNK)
-            s_t = stream.tile([P, PASSES, PACK, CHUNK], F32)
-            g_t = stream.tile([P, PASSES, PACK, CHUNK], BF16)
-            for h in halves:
-                for rows in pieces(c):
-                    nc.sync.dma_start(out=s_t[:, h, rows, :], in_=s_rows[h, :, rows, cols])
-                    nc.sync.dma_start(out=g_t[:, h, rows, :], in_=g_rows[h, :, rows, cols])
+            s_t = stream.tile([P, ROWS, CHUNK], F32)
+            g_t = stream.tile([P, ROWS, CHUNK], BF16)
+            for rows in pieces(c):
+                h = rows.start // PACK
+                inside = slice(rows.start - h * PACK, rows.stop - h * PACK)
+                nc.sync.dma_start(out=s_t[:, rows, :], in_=s_rows[h, :, inside, cols])
+                nc.sync.dma_start(out=g_t[:, rows, :], in_=g_rows[h, :, inside, cols])
             s_of[c] = s_t
             g_of[c] = g_t
 
@@ -125,165 +124,133 @@ def tile_capsulenetwork_pb_v_kernel(tc, p, Wr, s, grad_out, out):
 
         def square(c, h):
             if h == 0:
-                squares = work.tile([P, PASSES, PACK, CHUNK], F32, bufs=2)
+                squares = work.tile([P, ROWS, CHUNK], F32)
                 squares_of[c] = squares
             for rows in pieces(c):
-                nc.scalar.activation(
-                    out=squares_of[c][:, h, rows, :], in_=s_of[c][:, h, rows, :], func=ACT.Square
-                )
+                if rows.start // PACK == h:
+                    nc.scalar.activation(out=squares_of[c][:, rows, :], in_=s_of[c][:, rows, :], func=ACT.Square)
 
-        def multiply_g_s(engine, c, h, spans):
-            if (c, h) not in g_times_s_of:
-                g_times_s = work.tile([P, PACK, CHUNK], F32, name="product_%d" % h, bufs=1)
-                g_times_s_of[(c, h)] = g_times_s
-            for rows in spans:
-                engine.tensor_tensor(
-                    out=g_times_s_of[(c, h)][:, rows, :],
-                    in0=g_of[c][:, h, rows, :],
-                    in1=s_of[c][:, h, rows, :],
-                    op=ALU.mult,
-                )
+        def multiply_g_s(engine, c, first, last):
+            g_times_s = work.tile(
+                [P, last - first, CAP], F32, name="gpsimd_products" if first == 0 else "vector_products", bufs=1
+            )
+            engine.tensor_tensor(
+                out=g_times_s[:],
+                in0=by_capsule(g_of[c][:])[:, first:last],
+                in1=by_capsule(s_of[c][:])[:, first:last],
+                op=ALU.mult,
+            )
+            g_times_s_of.setdefault(c, []).append((g_times_s, first, last))
+
+        def multiply_first_g_s():
+            for engine, name, first in [(nc.gpsimd, "gpsimd_products", HALF), (nc.vector, "vector_products", 0)]:
+                g_times_s = work.tile([P, HALF, CAP], F32, name=name, bufs=1)
+                for x in [first, first + HALF // 2]:
+                    engine.tensor_tensor(
+                        out=g_times_s[:, x - first : x - first + HALF // 2],
+                        in0=by_capsule(g_of[0][:])[:, x : x + HALF // 2],
+                        in1=by_capsule(s_of[0][:])[:, x : x + HALF // 2],
+                        op=ALU.mult,
+                    )
+                g_times_s_of.setdefault(0, []).append((g_times_s, first, first + HALF))
 
         def sum_squares(c):
-            q = small.tile([P, PASSES * GROUPS], F32)
+            q = small.tile([P, GROUPS], F32)
             q_of[c] = q
-            if c > 0:
+            for rows in pieces(c) if c == 0 else [slice(0, ROWS)]:
                 nc.vector.tensor_reduce(
-                    out=q[:],
-                    in_=squares_of[c][:].rearrange("q h t (j o) -> q (h t j) o", o=CAP),
+                    out=q[:, rows.start * CAPSULES : rows.stop * CAPSULES],
+                    in_=by_capsule(squares_of[c][:, rows, :]),
                     axis=AXIS_X,
                     op=ALU.add,
                 )
-                return
-            for h in halves:
-                for rows in pieces(c):
-                    first = h * GROUPS + rows.start * CAPSULES
-                    nc.vector.tensor_reduce(
-                        out=q[:, first : first + (rows.stop - rows.start) * CAPSULES],
-                        in_=by_capsule(squares_of[c][:, h, rows, :]),
-                        axis=AXIS_X,
-                        op=ALU.add,
-                    )
 
         def functions_of_q(c):
             q = q_of[c]
-            r = small.tile([P, PASSES * GROUPS], F32)
+            r = small.tile([P, GROUPS], F32)
             nc.scalar.activation(out=r[:], in_=q[:], func=ACT.Abs_reciprocal_sqrt, bias=eps[:, 0:1])
-            q1_squared = small.tile([P, PASSES * GROUPS], F32)
+            q1_squared = small.tile([P, GROUPS], F32)
             nc.scalar.activation(out=q1_squared[:], in_=q[:], func=ACT.Square, bias=one[:, 0:1])
-            w = small.tile([P, PASSES * GROUPS], F32)
+            w = small.tile([P, GROUPS], F32)
             nc.scalar.activation(out=w[:], in_=q1_squared[:], func=ACT.Abs_reciprocal_sqrt)
-            eps_r2 = small.tile([P, PASSES * GROUPS], F32)
+            eps_r2 = small.tile([P, GROUPS], F32)
             nc.scalar.activation(out=eps_r2[:], in_=r[:], func=ACT.Square, scale=ROOT_EPS)
             r_of[c] = r
             w_of[c] = w
             eps_r2_of[c] = eps_r2
 
-        def sum_products(c, h):
-            if c not in d_of:
-                d = small.tile([P, PASSES * GROUPS], F32)
-                d_of[c] = d
-            d = d_of[c]
-            nc.vector.tensor_reduce(
-                out=d[:, h * GROUPS : (h + 1) * GROUPS],
-                in_=by_capsule(g_times_s_of[(c, h)][:]),
-                axis=AXIS_X,
-                op=ALU.add,
-            )
+        def sum_products(c):
+            d = small.tile([P, GROUPS], F32)
+            d_of[c] = d
+            for g_times_s, first, last in sorted(g_times_s_of[c], key=lambda part: -part[1]):
+                nc.vector.tensor_reduce(out=d[:, first:last], in_=g_times_s[:], axis=AXIS_X, op=ALU.add)
 
         def factors(c):
             q = q_of[c]
             w = w_of[c]
-            width = [P, PASSES * GROUPS]
+            width = [P, GROUPS]
             z = small.tile(width, F32)
             nc.vector.tensor_tensor(out=z[:], in0=w[:], in1=r_of[c][:], op=ALU.mult)
             bracket_1 = small.tile(width, F32)
             nc.vector.scalar_tensor_tensor(
                 out=bracket_1[:], in0=w[:], scalar=2.0, in1=eps_r2_of[c][:], op0=ALU.mult, op1=ALU.add
             )
-            z_d = work.tile(width, F32, name="product_0", bufs=1)
+            z_d = work.tile([P, GROUPS], F32, name="gpsimd_products", bufs=1)
             nc.vector.tensor_tensor(out=z_d[:], in0=z[:], in1=d_of[c][:], op=ALU.mult)
-            a_beta = small.tile([P, PASSES, 2, GROUPS], F32)
-            by_half = "q (h x) -> q h x"
-            nc.vector.tensor_tensor(
-                out=a_beta[:, :, 0, :],
-                in0=q[:].rearrange(by_half, h=PASSES),
-                in1=z[:].rearrange(by_half, h=PASSES),
-                op=ALU.mult,
-            )
+            a_beta = small.tile([P, 2, GROUPS], F32)
+            nc.vector.tensor_tensor(out=a_beta[:, 0, :], in0=q[:], in1=z[:], op=ALU.mult)
             nc.vector.scalar_tensor_tensor(
-                out=a_beta[:, :, 1, :],
-                in0=bracket_1[:].rearrange(by_half, h=PASSES),
-                scalar=-1.0,
-                in1=z_d[:].rearrange(by_half, h=PASSES),
-                op0=ALU.add,
-                op1=ALU.mult,
+                out=a_beta[:, 1, :], in0=bracket_1[:], scalar=-1.0, in1=z_d[:], op0=ALU.add, op1=ALU.mult
             )
-            a_psum = factor_banks.tile([P, PASSES, GROUPS], F32)
-            nc.tensor.matmul(out=a_psum[:], lhsT=identity[:], rhs=a_beta[:, :, 0, :], start=True, stop=True)
-            a_of[c] = a_psum
-            beta_psum = factor_banks.tile([P, PASSES, GROUPS], F32)
-            if c < CHUNKS - 1:
-                mine = (PACK - SCALAR_ROWS[0]) * CAPSULES
+            for k in range(2):
+                count = GROUPS if k == 0 else vector_scales(c)
+                factor = factor_banks.tile([P, GROUPS], F32, name="factor_%d" % k)
                 nc.tensor.matmul(
-                    out=beta_psum[:, 0, 0:mine],
-                    lhsT=identity[:],
-                    rhs=a_beta[:, 0, 1, 0:mine],
-                    start=True,
-                    stop=True,
+                    out=factor[:, 0:count], lhsT=identity[:], rhs=a_beta[:, k, 0:count], start=True, stop=True
                 )
-            else:
-                nc.tensor.matmul(
-                    out=beta_psum[:], lhsT=identity[:], rhs=a_beta[:, :, 1, :], start=True, stop=True
-                )
-            beta_of[c] = beta_psum
+                factor_of[(c, k)] = factor
             a_beta_of[c] = a_beta
 
+        def vector_scales(c):
+            return VECTOR_SCALES if c < CHUNKS - 1 else LAST_VECTOR_SCALES
+
         def scale_s_on_scalar(c):
-            for h in halves:
-                for t in range(PACK - scalar_rows(c, h), PACK):
-                    for j in range(CAPSULES):
-                        group = t * CAPSULES + j
-                        values = s_of[c][:, h, t, j * CAP : (j + 1) * CAP]
-                        nc.scalar.activation(
-                            out=values, in_=values, func=ACT.Copy, scale=a_beta_of[c][:, h, 1, group : group + 1]
-                        )
+            for x in range(vector_scales(c), GROUPS):
+                values = by_capsule(s_of[c][:])[:, x, :]
+                nc.scalar.activation(out=values, in_=values, func=ACT.Copy, scale=a_beta_of[c][:, 1, x : x + 1])
 
         def scale(c):
-            a_g = work.tile([P, PASSES, PACK, CHUNK], F32, bufs=1)
+            a_g = work.tile([P, ROWS, CHUNK], F32, bufs=1)
             a_g_of[c] = a_g
-            if c < CHUNKS - 1:
+            g = by_capsule(g_of[c][:])
+            s_t = by_capsule(s_of[c][:])
+            mine = vector_scales(c)
+            halved = [(0, HALF), (HALF, GROUPS)]
+            for first, last in [(0, GROUPS)] if c < CHUNKS - 1 else halved:
+                from_sbuf = c == CHUNKS - 1 and first == 0
+                a = a_beta_of[c][:, 0, :] if from_sbuf else factor_of[(c, 0)][:]
+                beta = a_beta_of[c][:, 1, :] if from_sbuf else factor_of[(c, 1)][:]
                 nc.vector.tensor_tensor(
-                    out=a_g[:].rearrange("q h t (j o) -> q (h t j) o", o=CAP),
-                    in0=g_of[c][:].rearrange("q h t (j o) -> q (h t j) o", o=CAP),
-                    in1=on_capsules(a_of[c][:].rearrange("q h x -> q (h x)"), PASSES * GROUPS),
+                    out=by_capsule(a_g[:])[:, first:last],
+                    in0=g[:, first:last],
+                    in1=on_capsules(a[:, first:last], last - first),
                     op=ALU.mult,
                 )
-            for h in halves:
-                if c == CHUNKS - 1:
-                    a, beta = (
-                        (a_beta_of[c][:, h, 0, :], a_beta_of[c][:, h, 1, :])
-                        if h == 0
-                        else (a_of[c][:, h, :], beta_of[c][:, h, :])
-                    )
-                    nc.vector.tensor_tensor(
-                        out=by_capsule(a_g[:, h]), in0=by_capsule(g_of[c][:, h]), in1=on_capsules(a, GROUPS), op=ALU.mult
-                    )
-                else:
-                    beta = beta_of[c][:, h, :]
-                rows = PACK - scalar_rows(c, h)
-                if rows > 0:
-                    mine = by_capsule(s_of[c][:, h, 0:rows, :])
-                    nc.vector.tensor_tensor(
-                        out=mine, in0=mine, in1=on_capsules(beta[:, 0 : rows * CAPSULES], rows * CAPSULES), op=ALU.mult
-                    )
+                last = min(last, mine)
+                nc.vector.tensor_tensor(
+                    out=s_t[:, first:last],
+                    in0=s_t[:, first:last],
+                    in1=on_capsules(beta[:, first:last], last - first),
+                    op=ALU.mult,
+                )
 
         def add(c, h):
             if h == 0:
                 ds_grouped = work.tile([P, PASSES, CHUNK, PACK], BF16, align_bytes=64)
                 grouped_of[c] = ds_grouped
-            a_g = a_g_of[c][:, h]
-            beta_s = s_of[c][:, h]
+            rows = slice(h * PACK, (h + 1) * PACK)
+            a_g = a_g_of[c][:, rows, :]
+            beta_s = s_of[c][:, rows, :]
             walk = "q (m w) t -> q w t m"
             natural = "q t (w m) -> q w t m"
             if (c, h) == (CHUNKS - 1, PASSES - 1):
@@ -364,29 +331,24 @@ def tile_capsulenetwork_pb_v_kernel(tc, p, Wr, s, grad_out, out):
         load(2)
         for h in halves:
             square(0, h)
-        multiply_g_s(nc.vector, 0, 0, pieces(0))
-        multiply_g_s(nc.gpsimd, 0, 1, pieces(0))
+        multiply_first_g_s()
         sum_squares(0)
         functions_of_q(0)
         for h in halves:
             square(1, h)
         for c in range(CHUNKS):
             more = c + 1 < CHUNKS
-            for h in reversed(halves):
-                sum_products(c, h)
-            if more:
-                multiply_g_s(nc.vector, c + 1, 1, [slice(0, VECTOR_ROWS)])
+            sum_products(c)
             factors(c)
             if more:
                 scale_s_on_scalar(c)
-                multiply_g_s(nc.gpsimd, c + 1, 0, [slice(0, PACK)])
-                if VECTOR_ROWS < PACK:
-                    multiply_g_s(nc.gpsimd, c + 1, 1, [slice(VECTOR_ROWS, PACK)])
+                multiply_g_s(nc.gpsimd, c + 1, 0, GPSIMD_PRODUCTS)
+                multiply_g_s(nc.vector, c + 1, GPSIMD_PRODUCTS, GROUPS)
             if c >= 2:
                 quantise(c - 2)
             if not more:
                 quantise(c - 1)
-            if c == 1:
+            if c == 2:
                 quantise_p()
             if c >= 2:
                 multiply(c - 2)

from contextlib import ExitStack

import concourse.mybir as mybir
from concourse.masks import make_identity

F32 = mybir.dt.float32
BF16 = mybir.dt.bfloat16
U32 = mybir.dt.uint32
U8 = mybir.dt.uint8
E4M3X4 = mybir.dt.float8_e4m3fn_x4
E5M2X4 = mybir.dt.float8_e5m2_x4
ACT = mybir.ActivationFunctionType
ALU = mybir.AluOpType
AXIS_X = mybir.AxisListType.X

P = 128
PACK = 4
BATCH = 1024
PASSES = BATCH // (P * PACK)
PRIMARY = 32
NI = PRIMARY * 16
CAP = 16
COLS = 256 * CAP
CHUNK = 512
CHUNKS = COLS // CHUNK
BLOCKS = CHUNK // P
CAPSULES = CHUNK // CAP
ROWS = PASSES * PACK
GROUPS = ROWS * CAPSULES
HALF = GROUPS // PASSES
VECTOR_SCALES = 96
LAST_VECTOR_SCALES = 192
GPSIMD_PRODUCTS = 192
GPSIMD_COLS = 384
SQ_EPS = 1e-8
ROOT_EPS = 1e-4
COUPLING = 1.0 / 256.0

FLOPS = 2 * BATCH * NI * COLS
BYTES = BATCH * NI * 2 + BATCH * COLS * (4 + 2) + NI * COLS * 4


def by_capsule(values):
    return values.rearrange("q r (j o) -> q (r j) o", o=CAP)


def on_capsules(factors, count):
    return factors.unsqueeze(2).to_broadcast([P, count, CAP])


def tile_capsulenetwork_pb_v_kernel(tc, p, Wr, s, grad_out, out):
    nc = tc.nc
    p_rows = p.rearrange("(h q t) n i -> h q t (n i)", h=PASSES, q=P, t=PACK)
    s_rows = s.rearrange("(h q t) j o -> h q t (j o)", h=PASSES, q=P, t=PACK)
    g_rows = grad_out.rearrange("(h q t) j o -> h q t (j o)", h=PASSES, q=P, t=PACK)
    out_chunks = out.rearrange("n j o i -> n (j o i)").rearrange(
        "n (c q x) -> c q n x", c=CHUNKS, q=P, x=BLOCKS * 16
    )
    halves = range(PASSES)

    with ExitStack() as stack:
        const = stack.enter_context(tc.tile_pool(name="const", bufs=1))
        stream = stack.enter_context(tc.tile_pool(name="stream", bufs=3))
        work = stack.enter_context(tc.tile_pool(name="work", bufs=2))
        small = stack.enter_context(tc.tile_pool(name="small", bufs=2))
        factor_banks = stack.enter_context(tc.psum_pool(name="factor_banks", bufs=1))
        product_banks = stack.enter_context(tc.psum_pool(name="product_banks", bufs=4))
        sum_banks = stack.enter_context(tc.psum_pool(name="sum_banks", bufs=2))
        stack.enter_context(tc.manual_schedule())

        s_of = {}
        g_of = {}
        squares_of = {}
        g_times_s_of = {}
        q_of = {}
        r_of = {}
        w_of = {}
        eps_r2_of = {}
        d_of = {}
        factor_of = {}
        a_beta_of = {}
        a_g_of = {}
        grouped_of = {}
        codes_of = {}
        scales_of = {}

        identity = const.tile([P, P], F32)
        make_identity(nc, identity[:])
        eps = const.tile([P, 1], F32)
        nc.vector.memset(eps[:], SQ_EPS)
        one = const.tile([P, 1], F32)
        nc.vector.memset(one[:], 1.0)
        p_raw = const.tile([P, PASSES, PACK, NI], BF16)
        p_grouped = const.tile([P, PASSES, NI, PACK], BF16, align_bytes=64)
        p_codes = const.tile([P, PASSES, NI], U32, align_bytes=64)
        p_scales = const.tile([P, PASSES, NI], U8, align_bytes=64)

        def pieces(c):
            step = PACK // 2 if c == 0 else PACK
            return [slice(r, r + step) for r in range(0, ROWS, step)]

        def load(c):
            cols = slice(c * CHUNK, (c + 1) * CHUNK)
            s_t = stream.tile([P, ROWS, CHUNK], F32)
            g_t = stream.tile([P, ROWS, CHUNK], BF16)
            for rows in pieces(c):
                h = rows.start // PACK
                inside = slice(rows.start - h * PACK, rows.stop - h * PACK)
                nc.sync.dma_start(out=s_t[:, rows, :], in_=s_rows[h, :, inside, cols])
                nc.sync.dma_start(out=g_t[:, rows, :], in_=g_rows[h, :, inside, cols])
            s_of[c] = s_t
            g_of[c] = g_t

        def regroup_p():
            for h in halves:
                nc.scalar.copy(out=p_grouped[:, h], in_=p_raw[:, h].rearrange("q t w -> q w t"))

        def quantise_p():
            nc.vector.quantize_mx(
                out=p_codes[:].rearrange("q h w -> q (h w)").bitcast(E4M3X4),
                scales=p_scales[:].rearrange("q h w -> q (h w)"),
                in_=p_grouped[:].rearrange("q h w t -> q (h w t)"),
            )

        def square(c, h):
            if h == 0:
                squares = work.tile([P, ROWS, CHUNK], F32)
                squares_of[c] = squares
            for rows in pieces(c):
                if rows.start // PACK == h:
                    nc.scalar.activation(out=squares_of[c][:, rows, :], in_=s_of[c][:, rows, :], func=ACT.Square)

        def multiply_g_s(engine, c, first, last):
            g_times_s = work.tile(
                [P, last - first, CAP], F32, name="gpsimd_products" if first == 0 else "vector_products", bufs=1
            )
            engine.tensor_tensor(
                out=g_times_s[:],
                in0=by_capsule(g_of[c][:])[:, first:last],
                in1=by_capsule(s_of[c][:])[:, first:last],
                op=ALU.mult,
            )
            g_times_s_of.setdefault(c, []).append((g_times_s, first, last))

        def multiply_first_g_s():
            for engine, name, first in [(nc.gpsimd, "gpsimd_products", HALF), (nc.vector, "vector_products", 0)]:
                g_times_s = work.tile([P, HALF, CAP], F32, name=name, bufs=1)
                for x in [first, first + HALF // 2]:
                    engine.tensor_tensor(
                        out=g_times_s[:, x - first : x - first + HALF // 2],
                        in0=by_capsule(g_of[0][:])[:, x : x + HALF // 2],
                        in1=by_capsule(s_of[0][:])[:, x : x + HALF // 2],
                        op=ALU.mult,
                    )
                g_times_s_of.setdefault(0, []).append((g_times_s, first, first + HALF))

        def sum_squares(c):
            q = small.tile([P, GROUPS], F32)
            q_of[c] = q
            for rows in pieces(c) if c == 0 else [slice(0, ROWS)]:
                nc.vector.tensor_reduce(
                    out=q[:, rows.start * CAPSULES : rows.stop * CAPSULES],
                    in_=by_capsule(squares_of[c][:, rows, :]),
                    axis=AXIS_X,
                    op=ALU.add,
                )

        def functions_of_q(c):
            q = q_of[c]
            r = small.tile([P, GROUPS], F32)
            nc.scalar.activation(out=r[:], in_=q[:], func=ACT.Abs_reciprocal_sqrt, bias=eps[:, 0:1])
            q1_squared = small.tile([P, GROUPS], F32)
            nc.scalar.activation(out=q1_squared[:], in_=q[:], func=ACT.Square, bias=one[:, 0:1])
            w = small.tile([P, GROUPS], F32)
            nc.scalar.activation(out=w[:], in_=q1_squared[:], func=ACT.Abs_reciprocal_sqrt)
            eps_r2 = small.tile([P, GROUPS], F32)
            nc.scalar.activation(out=eps_r2[:], in_=r[:], func=ACT.Square, scale=ROOT_EPS)
            r_of[c] = r
            w_of[c] = w
            eps_r2_of[c] = eps_r2

        def sum_products(c):
            d = small.tile([P, GROUPS], F32)
            d_of[c] = d
            for g_times_s, first, last in sorted(g_times_s_of[c], key=lambda part: -part[1]):
                nc.vector.tensor_reduce(out=d[:, first:last], in_=g_times_s[:], axis=AXIS_X, op=ALU.add)

        def factors(c):
            q = q_of[c]
            w = w_of[c]
            width = [P, GROUPS]
            z = small.tile(width, F32)
            nc.vector.tensor_tensor(out=z[:], in0=w[:], in1=r_of[c][:], op=ALU.mult)
            bracket_1 = small.tile(width, F32)
            nc.vector.scalar_tensor_tensor(
                out=bracket_1[:], in0=w[:], scalar=2.0, in1=eps_r2_of[c][:], op0=ALU.mult, op1=ALU.add
            )
            z_d = work.tile([P, GROUPS], F32, name="gpsimd_products", bufs=1)
            nc.vector.tensor_tensor(out=z_d[:], in0=z[:], in1=d_of[c][:], op=ALU.mult)
            a_beta = small.tile([P, 2, GROUPS], F32)
            nc.vector.tensor_tensor(out=a_beta[:, 0, :], in0=q[:], in1=z[:], op=ALU.mult)
            nc.vector.scalar_tensor_tensor(
                out=a_beta[:, 1, :], in0=bracket_1[:], scalar=-1.0, in1=z_d[:], op0=ALU.add, op1=ALU.mult
            )
            for k in range(2):
                count = GROUPS if k == 0 else vector_scales(c)
                factor = factor_banks.tile([P, GROUPS], F32, name="factor_%d" % k)
                nc.tensor.matmul(
                    out=factor[:, 0:count], lhsT=identity[:], rhs=a_beta[:, k, 0:count], start=True, stop=True
                )
                factor_of[(c, k)] = factor
            a_beta_of[c] = a_beta

        def vector_scales(c):
            return VECTOR_SCALES if c < CHUNKS - 1 else LAST_VECTOR_SCALES

        def scale_s_on_scalar(c):
            for x in range(vector_scales(c), GROUPS):
                values = by_capsule(s_of[c][:])[:, x, :]
                nc.scalar.activation(out=values, in_=values, func=ACT.Copy, scale=a_beta_of[c][:, 1, x : x + 1])

        def scale(c):
            a_g = work.tile([P, ROWS, CHUNK], F32, bufs=1)
            a_g_of[c] = a_g
            g = by_capsule(g_of[c][:])
            s_t = by_capsule(s_of[c][:])
            mine = vector_scales(c)
            halved = [(0, HALF), (HALF, GROUPS)]
            for first, last in [(0, GROUPS)] if c < CHUNKS - 1 else halved:
                from_sbuf = c == CHUNKS - 1 and first == 0
                a = a_beta_of[c][:, 0, :] if from_sbuf else factor_of[(c, 0)][:]
                beta = a_beta_of[c][:, 1, :] if from_sbuf else factor_of[(c, 1)][:]
                nc.vector.tensor_tensor(
                    out=by_capsule(a_g[:])[:, first:last],
                    in0=g[:, first:last],
                    in1=on_capsules(a[:, first:last], last - first),
                    op=ALU.mult,
                )
                last = min(last, mine)
                nc.vector.tensor_tensor(
                    out=s_t[:, first:last],
                    in0=s_t[:, first:last],
                    in1=on_capsules(beta[:, first:last], last - first),
                    op=ALU.mult,
                )

        def add(c, h):
            if h == 0:
                ds_grouped = work.tile([P, PASSES, CHUNK, PACK], BF16, align_bytes=64)
                grouped_of[c] = ds_grouped
            rows = slice(h * PACK, (h + 1) * PACK)
            a_g = a_g_of[c][:, rows, :]
            beta_s = s_of[c][:, rows, :]
            walk = "q (m w) t -> q w t m"
            natural = "q t (w m) -> q w t m"
            if (c, h) == (CHUNKS - 1, PASSES - 1):
                nc.vector.tensor_tensor(
                    out=grouped_of[c][:, h].rearrange("q (m w) t -> q m w t", m=BLOCKS),
                    in0=a_g.rearrange("q t (w m) -> q m w t", m=BLOCKS),
                    in1=beta_s.rearrange("q t (w m) -> q m w t", m=BLOCKS),
                    op=ALU.add,
                )
                return
            cols = GPSIMD_COLS if h == 0 else CHUNK
            nc.gpsimd.tensor_tensor(
                out=grouped_of[c][:, h].rearrange(walk, m=BLOCKS)[:, 0 : cols // BLOCKS],
                in0=a_g[:, :, 0:cols].rearrange(natural, m=BLOCKS),
                in1=beta_s[:, :, 0:cols].rearrange(natural, m=BLOCKS),
                op=ALU.add,
            )
            if cols < CHUNK:
                rest = sum_banks.tile([P, PACK, CHUNK - GPSIMD_COLS], F32)
                nc.tensor.matmul(out=rest[:], lhsT=identity[:], rhs=a_g[:, :, cols:CHUNK], start=True, stop=False)
                nc.tensor.matmul(out=rest[:], lhsT=identity[:], rhs=beta_s[:, :, cols:CHUNK], start=False, stop=True)
                nc.scalar.copy(
                    out=grouped_of[c][:, h].rearrange("q (m w) t -> q m w t", m=BLOCKS)[:, :, cols // BLOCKS : P, :],
                    in_=rest[:].rearrange("q t (w m) -> q m w t", m=BLOCKS),
                )

        def quantise(c):
            ds_codes = work.tile([P, PASSES, CHUNK], U32, align_bytes=64)
            ds_scales = work.tile([P, PASSES, CHUNK], U8, align_bytes=64)
            for hs in [halves] if c < CHUNKS - 1 else [halves[0:1], halves[1:2]]:
                span = slice(hs.start, hs.stop)
                nc.vector.quantize_mx(
                    out=ds_codes[:, span, :].rearrange("q h w -> q (h w)").bitcast(E5M2X4),
                    scales=ds_scales[:, span, :].rearrange("q h w -> q (h w)"),
                    in_=grouped_of[c][:, span].rearrange("q h w t -> q (h w t)"),
                )
            codes_of[c] = ds_codes
            scales_of[c] = ds_scales

        def multiply(c):
            result = work.tile([P, PRIMARY, BLOCKS, 16], F32)
            products = []
            for m in range(BLOCKS):
                product = product_banks.tile([P, NI], F32)
                products.append(product)
            for h in halves:
                for m in range(BLOCKS):
                    block = slice(m * P, (m + 1) * P)
                    nc.tensor.matmul_mx(
                        out=products[m][:],
                        lhsT=codes_of[c][:, h, block].bitcast(E5M2X4),
                        lhsT_scale=scales_of[c][:, h, block],
                        rhs=p_codes[:, h, :].bitcast(E4M3X4),
                        rhs_scale=p_scales[:, h, :],
                        start=(h == 0),
                        stop=(h == PASSES - 1),
                    )
            last = c == CHUNKS - 1
            stores = 2 if last else 1
            share = PRIMARY // stores
            for k in range(stores):
                capsules = slice(k * share, (k + 1) * share)
                for m in range(BLOCKS):
                    part = products[m][:].rearrange("q (n i) -> q n i", i=16)[:, capsules, :]
                    if last and m % 2 == 1:
                        nc.vector.tensor_scalar_mul(out=result[:, capsules, m, :], in0=part, scalar1=COUPLING)
                    else:
                        nc.scalar.mul(out=result[:, capsules, m, :], in_=part, mul=COUPLING)
                nc.sync.dma_start(
                    out=out_chunks[c][:, capsules, :],
                    in_=result[:, capsules, :, :].rearrange("q n m i -> q n (m i)"),
                )

        load(0)
        load(1)
        for h in halves:
            nc.sync.dma_start(out=p_raw[:, h], in_=p_rows[h])
        load(2)
        for h in halves:
            square(0, h)
        multiply_first_g_s()
        sum_squares(0)
        functions_of_q(0)
        for h in halves:
            square(1, h)
        for c in range(CHUNKS):
            more = c + 1 < CHUNKS
            sum_products(c)
            factors(c)
            if more:
                scale_s_on_scalar(c)
                multiply_g_s(nc.gpsimd, c + 1, 0, GPSIMD_PRODUCTS)
                multiply_g_s(nc.vector, c + 1, GPSIMD_PRODUCTS, GROUPS)
            if c >= 2:
                quantise(c - 2)
            if not more:
                quantise(c - 1)
            if c == 2:
                quantise_p()
            if c >= 2:
                multiply(c - 2)
            if not more:
                scale_s_on_scalar(c)
            scale(c)
            for h in halves:
                if (c, h) == (CHUNKS - 1, PASSES - 1):
                    multiply(c - 1)
                add(c, h)
            if more:
                sum_squares(c + 1)
            if c + 2 < CHUNKS:
                square(c + 2, 0)
            if more:
                functions_of_q(c + 1)
            if c == 0:
                regroup_p()
            if c + 2 < CHUNKS:
                square(c + 2, 1)
            if c + 3 < CHUNKS:
                load(c + 3)
        quantise(CHUNKS - 1)
        multiply(CHUNKS - 1)
